import numpy as np
import ml_dtypes


def mxq(x, axis, fmt="e4m3"):
    dtype, down = {"e4m3": (ml_dtypes.float8_e4m3fn, 7), "e5m2": (ml_dtypes.float8_e5m2, 14)}[fmt]
    v = np.moveaxis(np.asarray(x, np.float32).astype(ml_dtypes.bfloat16).astype(np.float64), axis, -1)
    blocks = v.reshape(v.shape[:-1] + (-1, 32))
    amax = np.abs(blocks).max(-1, keepdims=True)
    byte = np.maximum(np.where(amax > 0, np.frexp(amax)[1] - 1 + 127, 0) - down, 1)
    scale = np.exp2(byte - 127.0)
    codes = (blocks / scale).astype(np.float32).astype(dtype).astype(np.float64)
    return np.moveaxis((codes * scale).reshape(v.shape), -1, axis)


WIDE = False


def mx_kscale(k):
    if not WIDE:
        return np.ones(k)
    levels = np.array([10, -10, 5, -5, 0])
    a = np.random.permutation(np.resize(levels, k // 512 * 4)).reshape(k // 512, 4)
    idx = np.arange(k)
    return np.exp2(a[idx // 512, idx % 128 // 32])


BF16 = ml_dtypes.bfloat16


def bf(x):
    return np.asarray(x, np.float32).astype(BF16)


def f64(x):
    return np.asarray(x).astype(np.float64)


B, I, O, NUM, KO = 4096, 512, 128, 8, 3
G = NUM + KO


def silu(v):
    e = np.exp(-np.abs(v))
    return v * np.where(v >= 0, 1.0, e) / (1.0 + e)


def extend_grid(grid, k):
    h = (grid[:, -1:] - grid[:, :1]) / (grid.shape[1] - 1)
    for _ in range(k):
        grid = np.concatenate([grid[:, :1] - h, grid, grid[:, -1:] + h], axis=1)
    return grid


def b_batch(x, grid, k):
    xg = x[:, :, None]
    g = grid[None, :, :]
    value = ((xg >= g[:, :, :-1]) & (xg < g[:, :, 1:])).astype(np.float64)
    for p in range(1, k + 1):
        value = (xg - g[:, :, :-(p + 1)]) / (g[:, :, p:-1] - g[:, :, :-(p + 1)]) * value[:, :, :-1] \
              + (g[:, :, p + 1:] - xg) / (g[:, :, p + 1:] - g[:, :, 1:-p]) * value[:, :, 1:]
        value = np.nan_to_num(value)
    return value


def setup_inputs():
    s = mx_kscale(I)
    x = np.random.uniform(-1.0, 1.0, (B, I))
    lo = -1.0 - 0.2 * np.random.random((I, 1))
    hi = 1.0 + 0.2 * np.random.random((I, 1))
    base_grid = lo + (hi - lo) * np.linspace(0.0, 1.0, NUM + 1)[None, :]
    grid = extend_grid(base_grid, KO)
    return {"x": bf(x * s),
            "grid": bf(grid * s[:, None]),
            "coef": bf(np.random.standard_normal((I, O, G))),
            "scale_base": bf(np.random.standard_normal((I, O)) * 2.0 / np.sqrt(I) / s[:, None]),
            "scale_sp": bf((1.0 + 0.1 * np.random.standard_normal((I, O))) / np.sqrt(I)),
            "mask": bf(1.0 + 0.1 * np.random.standard_normal((I, O)))}


def reference(x, grid, coef, scale_base, scale_sp, mask):
    x, grid, coef = f64(x), f64(grid), f64(coef)
    scale_base, scale_sp, mask = f64(scale_base), f64(scale_sp), f64(mask)
    base = silu(x)
    bs = b_batch(x, grid, KO)
    ws = coef * (mask * scale_sp)[:, :, None]
    out_spline = (mxq(bs.transpose(2, 0, 1), 2, "e4m3") @ mxq(ws.transpose(2, 0, 1), 1, "e4m3")).sum(0)
    out_base = mxq(base, 1, "e4m3") @ mxq(mask * scale_base, 0, "e4m3")
    return out_base + out_spline

@@ -1,0 +1,235 @@
+from contextlib import ExitStack
+
+import concourse.mybir as mybir
+from concourse.masks import make_identity
+
+F32 = mybir.dt.float32
+BF16 = mybir.dt.bfloat16
+U32 = mybir.dt.uint32
+U8 = mybir.dt.uint8
+FP8X4 = mybir.dt.float8_e4m3fn_x4
+ACT = mybir.ActivationFunctionType
+ALU = mybir.AluOpType
+
+B, I, O, G, NK = 4096, 512, 128, 11, 15
+P = 128
+U = I // P
+NB = 1024
+NT = NB // P
+NCH = B // NB
+NPL = G + 1
+HALF = 512
+SPLIT = 768
+RUN = 4
+
+FLOPS = 2 * B * I * O * NPL
+
+
+def tile_kan_layer_t_kernel(tc, x, grid, coef, scale_base, scale_sp, mask, out):
+    nc = tc.nc
+    with ExitStack() as ctx:
+        const = ctx.enter_context(tc.tile_pool(name="const", bufs=1))
+        xs_pool = ctx.enter_context(tc.tile_pool(name="xs", bufs=1))
+        t_pool = ctx.enter_context(tc.tile_pool(name="t", bufs=2))
+        tp_psum = ctx.enter_context(tc.psum_pool(name="tp", bufs=2))
+
+        ident_bf = const.tile([P, P], BF16)
+        make_identity(nc, ident_bf[:])
+        ident_f = const.tile([P, P], F32)
+        make_identity(nc, ident_f[:])
+
+        g_bf = const.tile([P, U, NK], BF16)
+        nc.sync.dma_start(out=g_bf[:], in_=grid.rearrange("(u p) j -> p u j", p=P))
+
+        def load_chunk(c):
+            xs = xs_pool.tile([P, NT, I], BF16)
+            nc.sync.dma_start(out=xs[:], in_=x[c * NB : (c + 1) * NB, :].rearrange("(p n) i -> p n i", n=NT))
+            t = t_pool.tile([P, U, NB], BF16)
+            for u in range(U):
+                tp = tp_psum.tile([P, NB], BF16)
+                for n in range(NT):
+                    nc.tensor.transpose(tp[:, n * P : (n + 1) * P], xs[:, n, u * P : (u + 1) * P], ident_bf[:])
+                nc.scalar.copy(out=t[:, u, :], in_=tp[:])
+            return t
+
+        t_next = load_chunk(0)
+
+        g = const.tile([P, U, NK], F32)
+        nc.vector.tensor_copy(out=g[:], in_=g_bf[:])
+        neg_g = const.tile([P, U, NK], F32)
+        nc.vector.tensor_scalar_mul(out=neg_g[:], in0=g[:], scalar1=-1.0)
+        d1 = const.tile([P, U, NK - 1], F32)
+        nc.vector.tensor_sub(out=d1[:], in0=g[:, :, 1:NK], in1=g[:, :, 0 : NK - 1])
+        d2 = const.tile([P, U, NK - 2], F32)
+        nc.vector.tensor_sub(out=d2[:], in0=g[:, :, 2:NK], in1=g[:, :, 0 : NK - 2])
+        d3 = const.tile([P, U, NK - 3], F32)
+        nc.vector.tensor_sub(out=d3[:], in0=g[:, :, 3:NK], in1=g[:, :, 0 : NK - 3])
+        d4 = const.tile([P, U, NK - 4], F32)
+        nc.vector.tensor_sub(out=d4[:], in0=g[:, :, 4:NK], in1=g[:, :, 0 : NK - 4])
+
+        def product(name, factors):
+            acc = const.tile([P, U, G], F32, name=name)
+            nc.vector.tensor_mul(out=acc[:], in0=factors[0], in1=factors[1])
+            for f in factors[2:]:
+                nc.vector.tensor_mul(out=acc[:], in0=acc[:], in1=f)
+            return acc
+
+        c0 = product("c0", [d1[:, :, 0:G], d2[:, :, 0:G], d3[:, :, 0:G]])
+        nc.vector.reciprocal(out=c0[:], in_=c0[:])
+        c1 = product("c1", [d1[:, :, 0:G], d1[:, :, 1 : G + 1], d2[:, :, 1 : G + 1], d3[:, :, 1 : G + 1]])
+        nc.vector.reciprocal(out=c1[:], in_=c1[:])
+        nc.vector.tensor_mul(out=c1[:], in0=c1[:], in1=d4[:])
+        e4 = product("e4", [d3[:, :, 1 : G + 1], d2[:, :, 2 : G + 2], d1[:, :, 3 : G + 3]])
+        nc.vector.reciprocal(out=e4[:], in_=e4[:])
+        nc.vector.tensor_scalar_mul(out=e4[:], in0=e4[:], scalar1=-1.0)
+        e3 = product("e3", [d3[:, :, 0:G], d2[:, :, 1 : G + 1], d1[:, :, 2 : G + 2], d1[:, :, 3 : G + 3]])
+        nc.vector.reciprocal(out=e3[:], in_=e3[:])
+        nc.vector.tensor_mul(out=e3[:], in0=e3[:], in1=d4[:])
+        nc.vector.tensor_scalar_mul(out=e3[:], in0=e3[:], scalar1=-1.0)
+
+        w_codes = const.tile([P, NPL * O], U32, align_bytes=64)
+        w_scales = const.tile([P, NPL * O], U8, align_bytes=64)
+        with tc.tile_pool(name="wprep", bufs=1) as wprep:
+            mask_sb = wprep.tile([P, U, O], BF16)
+            nc.sync.dma_start(out=mask_sb[:], in_=mask.rearrange("(u p) o -> p u o", p=P))
+            sp_sb = wprep.tile([P, U, O], BF16)
+            nc.sync.dma_start(out=sp_sb[:], in_=scale_sp.rearrange("(u p) o -> p u o", p=P))
+            base_sb = wprep.tile([P, U, O], BF16)
+            nc.sync.dma_start(out=base_sb[:], in_=scale_base.rearrange("(u p) o -> p u o", p=P))
+            coef_sb = wprep.tile([P, U, O * G], BF16)
+            nc.sync.dma_start(out=coef_sb[:], in_=coef.rearrange("(u p) o k -> p u (o k)", p=P))
+            msp = wprep.tile([P, U, O], F32)
+            nc.vector.tensor_mul(out=msp[:], in0=mask_sb[:], in1=sp_sb[:])
+            w_grouped = wprep.tile([P, NPL, O, U], BF16, align_bytes=64)
+            coef_v = coef_sb[:].rearrange("p u (o k) -> p k o u", k=G)
+            for k in range(G):
+                nc.vector.tensor_tensor(
+                    out=w_grouped[:, k, :, :], in0=coef_v[:, k, :, :], in1=msp[:].rearrange("p u o -> p o u"), op=ALU.mult
+                )
+            nc.vector.tensor_tensor(
+                out=w_grouped[:, G, :, :],
+                in0=mask_sb[:].rearrange("p u o -> p o u"),
+                in1=base_sb[:].rearrange("p u o -> p o u"),
+                op=ALU.mult,
+            )
+            w_flat = w_grouped[:].rearrange("p k o u -> p (k o u)")
+            nc.vector.quantize_mx(
+                out=w_codes[:, 0:1024].bitcast(FP8X4), scales=w_scales[:, 0:1024], in_=w_flat[:, 0:4096]
+            )
+            nc.vector.quantize_mx(
+                out=w_codes[:, 1024:1536].bitcast(FP8X4), scales=w_scales[:, 1024:1536], in_=w_flat[:, 4096:6144]
+            )
+
+        s_pool = ctx.enter_context(tc.tile_pool(name="s", bufs=3))
+        sq_pool = ctx.enter_context(tc.tile_pool(name="sq", bufs=3))
+        in_pool = ctx.enter_context(tc.tile_pool(name="inner", bufs=3))
+        left_pool = ctx.enter_context(tc.tile_pool(name="left", bufs=5))
+        right_pool = ctx.enter_context(tc.tile_pool(name="right", bufs=2))
+        grp_pool = ctx.enter_context(tc.tile_pool(name="grp", bufs=3))
+        q_pool = ctx.enter_context(tc.tile_pool(name="q", bufs=2))
+        o_pool = ctx.enter_context(tc.tile_pool(name="o", bufs=1))
+        acc_psum = ctx.enter_context(tc.psum_pool(name="acc", bufs=2))
+        ot_psum = ctx.enter_context(tc.psum_pool(name="ot", bufs=2))
+
+        def by_runs_dst(grouped, lo, hi):
+            return grouped[:, lo:hi, :].rearrange("p (c r) u -> p c u r", r=RUN)
+
+        def by_runs_src(plane, lo, hi):
+            return plane[:, :, lo:hi].rearrange("p u (c r) -> p c u r", r=RUN)
+
+        def quantise_and_multiply(grouped, plane, acc):
+            codes = q_pool.tile([P, NB], U32, align_bytes=64)
+            scales = q_pool.tile([P, NB], U8, align_bytes=64)
+            nc.vector.quantize_mx(
+                out=codes[:].bitcast(FP8X4), scales=scales[:], in_=grouped[:].rearrange("p b u -> p (b u)")
+            )
+            w_cols = slice(plane * O, (plane + 1) * O)
+            for h in range(NB // HALF):
+                cols = slice(h * HALF, (h + 1) * HALF)
+                nc.tensor.matmul_mx(
+                    out=acc[h][:],
+                    lhsT=w_codes[:, w_cols].bitcast(FP8X4),
+                    lhsT_scale=w_scales[:, w_cols],
+                    rhs=codes[:, cols].bitcast(FP8X4),
+                    rhs_scale=scales[:, cols],
+                    start=(plane == G),
+                    stop=(plane == G - 1),
+                )
+
+        for c in range(NCH):
+            t = t_next
+            acc0 = acc_psum.tile([P, HALF], F32)
+            acc1 = acc_psum.tile([P, HALF], F32)
+            acc = [acc0, acc1]
+
+            base_grouped = grp_pool.tile([P, NB, U], BF16, tag="grp", align_bytes=64)
+            nc.scalar.activation(out=by_runs_dst(base_grouped, 0, NB), in_=by_runs_src(t, 0, NB), func=ACT.Silu)
+            waiting = (base_grouped, G)
+
+            lefts = {}
+            s_prev = None
+            for j in range(NK):
+                s_cur = s_pool.tile([P, U, NB], F32)
+                for u in range(U):
+                    sq = sq_pool.tile([P, NB], F32)
+                    nc.scalar.activation(
+                        out=sq[:], in_=t[:, u, :], func=ACT.Square, bias=neg_g[:, u, j : j + 1], scale=1.0
+                    )
+                    nc.vector.scalar_tensor_tensor(
+                        out=s_cur[:, u, :], in0=t[:, u, :], scalar=g[:, u, j : j + 1], in1=sq[:],
+                        op0=ALU.subtract, op1=ALU.mult,
+                    )
+                if 1 <= j <= G:
+                    k = j - 1
+                    left = left_pool.tile([P, U, NB], BF16)
+                    lefts[k] = left
+                    for u in range(U):
+                        left_in = in_pool.tile([P, NB], F32)
+                        nc.scalar.activation(
+                            out=left_in[:], in_=s_cur[:, u, :], func=ACT.Relu, scale=c1[:, u, k : k + 1]
+                        )
+                        nc.vector.scalar_tensor_tensor(
+                            out=left[:, u, :], in0=s_prev[:, u, :], scalar=c0[:, u, k : k + 1], in1=left_in[:],
+                            op0=ALU.mult, op1=ALU.subtract,
+                        )
+                if j >= 4:
+                    k = j - 4
+                    right = right_pool.tile([P, U, NB], BF16)
+                    for u in range(U):
+                        right_in = in_pool.tile([P, NB], F32)
+                        nc.scalar.activation(
+                            out=right_in[:], in_=s_prev[:, u, :], func=ACT.Relu, scale=e3[:, u, k : k + 1]
+                        )
+                        nc.vector.scalar_tensor_tensor(
+                            out=right[:, u, :], in0=s_cur[:, u, :], scalar=e4[:, u, k : k + 1], in1=right_in[:],
+                            op0=ALU.mult, op1=ALU.subtract,
+                        )
+                    nc.vector.tensor_tensor(out=right[:], in0=lefts[k][:], in1=right[:], op=ALU.max)
+                    quantise_and_multiply(waiting[0], waiting[1], acc)
+                    grouped = grp_pool.tile([P, NB, U], BF16, tag="grp", align_bytes=64)
+                    nc.scalar.activation(
+                        out=by_runs_dst(grouped, 0, SPLIT), in_=by_runs_src(right, 0, SPLIT), func=ACT.Relu
+                    )
+                    nc.vector.tensor_scalar_max(
+                        out=by_runs_dst(grouped, SPLIT, NB), in0=by_runs_src(right, SPLIT, NB), scalar1=0.0
+                    )
+                    waiting = (grouped, k)
+                s_prev = s_cur
+                if j == 8 and c + 1 < NCH:
+                    t_next = load_chunk(c + 1)
+            quantise_and_multiply(waiting[0], waiting[1], acc)
+
+            out_t = o_pool.tile([P, NB], F32)
+            nc.scalar.copy(out=out_t[:, 0:HALF], in_=acc0[:])
+            nc.vector.tensor_copy(out=out_t[:, HALF:NB], in_=acc1[:])
+            out_sb = o_pool.tile([P, NT, O], F32)
+            for h in range(NB // HALF):
+                ot = ot_psum.tile([P, 4, O], F32)
+                for q in range(4):
+                    n = h * 4 + q
+                    nc.tensor.transpose(ot[:, q, :], out_t[:, n * P : (n + 1) * P], ident_f[:])
+                if h == 0:
+                    nc.scalar.copy(out=out_sb[:, 0:4, :], in_=ot[:])
+                else:
+                    nc.vector.tensor_copy(out=out_sb[:, 4:8, :], in_=ot[:])
+            nc.sync.dma_start(out=out[c * NB : (c + 1) * NB, :].rearrange("(p n) o -> p n o", n=NT), in_=out_sb[:])

@@ -19,8 +19,8 @@ NT = NB // P
 NCH = B // NB
 NPL = G + 1
 HALF = 512
-SPLIT = 768
 RUN = 4
+SPLIT = {0:512,5:352,6:1024,7:864,8:864,9:704,10:704,11:864,12:864,13:864,14:864}
 
 FLOPS = 2 * B * I * O * NPL
 
@@ -28,10 +28,22 @@ FLOPS = 2 * B * I * O * NPL
 def tile_kan_layer_t_kernel(tc, x, grid, coef, scale_base, scale_sp, mask, out):
     nc = tc.nc
     with ExitStack() as ctx:
+        ctx.enter_context(tc.manual_schedule())
         const = ctx.enter_context(tc.tile_pool(name="const", bufs=1))
+        wprep = ctx.enter_context(tc.tile_pool(name="wprep", bufs=1))
         xs_pool = ctx.enter_context(tc.tile_pool(name="xs", bufs=1))
         t_pool = ctx.enter_context(tc.tile_pool(name="t", bufs=2))
+        s_pool = ctx.enter_context(tc.tile_pool(name="s", bufs=2))
+        sq_pool = ctx.enter_context(tc.tile_pool(name="sq", bufs=4))
+        in_pool = ctx.enter_context(tc.tile_pool(name="inner", bufs=4))
+        left_pool = ctx.enter_context(tc.tile_pool(name="left", bufs=4))
+        right_pool = ctx.enter_context(tc.tile_pool(name="right", bufs=2))
+        grp_pool = ctx.enter_context(tc.tile_pool(name="grp", bufs=3))
+        q_pool = ctx.enter_context(tc.tile_pool(name="q", bufs=2))
+        o_pool = ctx.enter_context(tc.tile_pool(name="o", bufs=1))
         tp_psum = ctx.enter_context(tc.psum_pool(name="tp", bufs=2))
+        acc_psum = ctx.enter_context(tc.psum_pool(name="acc", bufs=2))
+        ot_psum = ctx.enter_context(tc.psum_pool(name="ot", bufs=2))
 
         ident_bf = const.tile([P, P], BF16)
         make_identity(nc, ident_bf[:])
@@ -41,23 +53,37 @@ def tile_kan_layer_t_kernel(tc, x, grid, coef, scale_base, scale_sp, mask, out):
         g_bf = const.tile([P, U, NK], BF16)
         nc.sync.dma_start(out=g_bf[:], in_=grid.rearrange("(u p) j -> p u j", p=P))
 
-        def load_chunk(c):
+        def load_x(c):
             xs = xs_pool.tile([P, NT, I], BF16)
             nc.sync.dma_start(out=xs[:], in_=x[c * NB : (c + 1) * NB, :].rearrange("(p n) i -> p n i", n=NT))
-            t = t_pool.tile([P, U, NB], BF16)
-            for u in range(U):
-                tp = tp_psum.tile([P, NB], BF16)
-                for n in range(NT):
-                    nc.tensor.transpose(tp[:, n * P : (n + 1) * P], xs[:, n, u * P : (u + 1) * P], ident_bf[:])
-                nc.scalar.copy(out=t[:, u, :], in_=tp[:])
-            return t
+            return xs
 
-        t_next = load_chunk(0)
+        def turn_x(xs, u):
+            tp = tp_psum.tile([P, NB], BF16)
+            for n in range(NT):
+                nc.tensor.transpose(tp[:, n * P : (n + 1) * P], xs[:, n, u * P : (u + 1) * P], ident_bf[:])
+            return tp
+
+        xs0 = load_x(0)
+        mask_sb = wprep.tile([P, U, O], BF16)
+        nc.sync.dma_start(out=mask_sb[:], in_=mask.rearrange("(u p) o -> p u o", p=P))
+        sp_sb = wprep.tile([P, U, O], BF16)
+        nc.sync.dma_start(out=sp_sb[:], in_=scale_sp.rearrange("(u p) o -> p u o", p=P))
+        base_sb = wprep.tile([P, U, O], BF16)
+        nc.sync.dma_start(out=base_sb[:], in_=scale_base.rearrange("(u p) o -> p u o", p=P))
+        coef_sb = wprep.tile([P, U, O * G], BF16)
+        nc.sync.dma_start(out=coef_sb[:], in_=coef.rearrange("(u p) o k -> p u (o k)", p=P))
 
         g = const.tile([P, U, NK], F32)
         nc.vector.tensor_copy(out=g[:], in_=g_bf[:])
         neg_g = const.tile([P, U, NK], F32)
         nc.vector.tensor_scalar_mul(out=neg_g[:], in0=g[:], scalar1=-1.0)
+
+        t_first = t_pool.tile([P, U, NB], BF16, tag="t")
+        for u in range(U):
+            tp0 = turn_x(xs0, u)
+            nc.scalar.copy(out=t_first[:, u, :], in_=tp0[:])
+
         d1 = const.tile([P, U, NK - 1], F32)
         nc.vector.tensor_sub(out=d1[:], in0=g[:, :, 1:NK], in1=g[:, :, 0 : NK - 1])
         d2 = const.tile([P, U, NK - 2], F32)
@@ -89,47 +115,33 @@ def tile_kan_layer_t_kernel(tc, x, grid, coef, scale_base, scale_sp, mask, out):
 
         w_codes = const.tile([P, NPL * O], U32, align_bytes=64)
         w_scales = const.tile([P, NPL * O], U8, align_bytes=64)
-        with tc.tile_pool(name="wprep", bufs=1) as wprep:
-            mask_sb = wprep.tile([P, U, O], BF16)
-            nc.sync.dma_start(out=mask_sb[:], in_=mask.rearrange("(u p) o -> p u o", p=P))
-            sp_sb = wprep.tile([P, U, O], BF16)
-            nc.sync.dma_start(out=sp_sb[:], in_=scale_sp.rearrange("(u p) o -> p u o", p=P))
-            base_sb = wprep.tile([P, U, O], BF16)
-            nc.sync.dma_start(out=base_sb[:], in_=scale_base.rearrange("(u p) o -> p u o", p=P))
-            coef_sb = wprep.tile([P, U, O * G], BF16)
-            nc.sync.dma_start(out=coef_sb[:], in_=coef.rearrange("(u p) o k -> p u (o k)", p=P))
+
+        def prepare_weights():
             msp = wprep.tile([P, U, O], F32)
             nc.vector.tensor_mul(out=msp[:], in0=mask_sb[:], in1=sp_sb[:])
-            w_grouped = wprep.tile([P, NPL, O, U], BF16, align_bytes=64)
             coef_v = coef_sb[:].rearrange("p u (o k) -> p k o u", k=G)
-            for k in range(G):
-                nc.vector.tensor_tensor(
-                    out=w_grouped[:, k, :, :], in0=coef_v[:, k, :, :], in1=msp[:].rearrange("p u o -> p o u"), op=ALU.mult
+            for first, count in ((0, 8), (8, 4)):
+                w_grouped = grp_pool.tile([P, NB, U], BF16, tag="grp", align_bytes=64)
+                w_flat = w_grouped[:].rearrange("p b u -> p (b u)")
+                for n in range(count):
+                    plane = first + n
+                    dst = w_flat[:, n * O * U : (n + 1) * O * U].rearrange("p (o u) -> p o u", u=U)
+                    if plane < G:
+                        nc.vector.tensor_tensor(
+                            out=dst, in0=coef_v[:, plane, :, :], in1=msp[:].rearrange("p u o -> p o u"), op=ALU.mult
+                        )
+                    else:
+                        nc.vector.tensor_tensor(
+                            out=dst,
+                            in0=mask_sb[:].rearrange("p u o -> p o u"),
+                            in1=base_sb[:].rearrange("p u o -> p o u"),
+                            op=ALU.mult,
+                        )
+                nc.vector.quantize_mx(
+                    out=w_codes[:, first * O : (first + count) * O].bitcast(FP8X4),
+                    scales=w_scales[:, first * O : (first + count) * O],
+                    in_=w_flat[:, 0 : count * O * U],
                 )
-            nc.vector.tensor_tensor(
-                out=w_grouped[:, G, :, :],
-                in0=mask_sb[:].rearrange("p u o -> p o u"),
-                in1=base_sb[:].rearrange("p u o -> p o u"),
-                op=ALU.mult,
-            )
-            w_flat = w_grouped[:].rearrange("p k o u -> p (k o u)")
-            nc.vector.quantize_mx(
-                out=w_codes[:, 0:1024].bitcast(FP8X4), scales=w_scales[:, 0:1024], in_=w_flat[:, 0:4096]
-            )
-            nc.vector.quantize_mx(
-                out=w_codes[:, 1024:1536].bitcast(FP8X4), scales=w_scales[:, 1024:1536], in_=w_flat[:, 4096:6144]
-            )
-
-        s_pool = ctx.enter_context(tc.tile_pool(name="s", bufs=3))
-        sq_pool = ctx.enter_context(tc.tile_pool(name="sq", bufs=3))
-        in_pool = ctx.enter_context(tc.tile_pool(name="inner", bufs=3))
-        left_pool = ctx.enter_context(tc.tile_pool(name="left", bufs=5))
-        right_pool = ctx.enter_context(tc.tile_pool(name="right", bufs=2))
-        grp_pool = ctx.enter_context(tc.tile_pool(name="grp", bufs=3))
-        q_pool = ctx.enter_context(tc.tile_pool(name="q", bufs=2))
-        o_pool = ctx.enter_context(tc.tile_pool(name="o", bufs=1))
-        acc_psum = ctx.enter_context(tc.psum_pool(name="acc", bufs=2))
-        ot_psum = ctx.enter_context(tc.psum_pool(name="ot", bufs=2))
 
         def by_runs_dst(grouped, lo, hi):
             return grouped[:, lo:hi, :].rearrange("p (c r) u -> p c u r", r=RUN)
@@ -156,80 +168,145 @@ def tile_kan_layer_t_kernel(tc, x, grid, coef, scale_base, scale_sp, mask, out):
                     stop=(plane == G - 1),
                 )
 
-        for c in range(NCH):
-            t = t_next
-            acc0 = acc_psum.tile([P, HALF], F32)
-            acc1 = acc_psum.tile([P, HALF], F32)
-            acc = [acc0, acc1]
+        def regroup(plane_tile, split):
+            grouped = grp_pool.tile([P, NB, U], BF16, tag="grp", align_bytes=64)
+            if split > 0:
+                nc.scalar.activation(
+                    out=by_runs_dst(grouped, 0, split), in_=by_runs_src(plane_tile, 0, split), func=ACT.Relu
+                )
+            if split < NB:
+                nc.vector.tensor_scalar_max(
+                    out=by_runs_dst(grouped, split, NB), in0=by_runs_src(plane_tile, split, NB), scalar1=0.0
+                )
+            return grouped
 
-            base_grouped = grp_pool.tile([P, NB, U], BF16, tag="grp", align_bytes=64)
-            nc.scalar.activation(out=by_runs_dst(base_grouped, 0, NB), in_=by_runs_src(t, 0, NB), func=ACT.Silu)
-            waiting = (base_grouped, G)
-
-            lefts = {}
-            s_prev = None
-            for j in range(NK):
-                s_cur = s_pool.tile([P, U, NB], F32)
-                for u in range(U):
-                    sq = sq_pool.tile([P, NB], F32)
-                    nc.scalar.activation(
-                        out=sq[:], in_=t[:, u, :], func=ACT.Square, bias=neg_g[:, u, j : j + 1], scale=1.0
-                    )
-                    nc.vector.scalar_tensor_tensor(
-                        out=s_cur[:, u, :], in0=t[:, u, :], scalar=g[:, u, j : j + 1], in1=sq[:],
-                        op0=ALU.subtract, op1=ALU.mult,
-                    )
-                if 1 <= j <= G:
-                    k = j - 1
-                    left = left_pool.tile([P, U, NB], BF16)
-                    lefts[k] = left
-                    for u in range(U):
-                        left_in = in_pool.tile([P, NB], F32)
-                        nc.scalar.activation(
-                            out=left_in[:], in_=s_cur[:, u, :], func=ACT.Relu, scale=c1[:, u, k : k + 1]
-                        )
-                        nc.vector.scalar_tensor_tensor(
-                            out=left[:, u, :], in0=s_prev[:, u, :], scalar=c0[:, u, k : k + 1], in1=left_in[:],
-                            op0=ALU.mult, op1=ALU.subtract,
-                        )
-                if j >= 4:
-                    k = j - 4
-                    right = right_pool.tile([P, U, NB], BF16)
-                    for u in range(U):
-                        right_in = in_pool.tile([P, NB], F32)
-                        nc.scalar.activation(
-                            out=right_in[:], in_=s_prev[:, u, :], func=ACT.Relu, scale=e3[:, u, k : k + 1]
-                        )
-                        nc.vector.scalar_tensor_tensor(
-                            out=right[:, u, :], in0=s_cur[:, u, :], scalar=e4[:, u, k : k + 1], in1=right_in[:],
-                            op0=ALU.mult, op1=ALU.subtract,
-                        )
-                    nc.vector.tensor_tensor(out=right[:], in0=lefts[k][:], in1=right[:], op=ALU.max)
-                    quantise_and_multiply(waiting[0], waiting[1], acc)
-                    grouped = grp_pool.tile([P, NB, U], BF16, tag="grp", align_bytes=64)
-                    nc.scalar.activation(
-                        out=by_runs_dst(grouped, 0, SPLIT), in_=by_runs_src(right, 0, SPLIT), func=ACT.Relu
-                    )
-                    nc.vector.tensor_scalar_max(
-                        out=by_runs_dst(grouped, SPLIT, NB), in0=by_runs_src(right, SPLIT, NB), scalar1=0.0
-                    )
-                    waiting = (grouped, k)
-                s_prev = s_cur
-                if j == 8 and c + 1 < NCH:
-                    t_next = load_chunk(c + 1)
-            quantise_and_multiply(waiting[0], waiting[1], acc)
-
+        def empty_sums(acc):
             out_t = o_pool.tile([P, NB], F32)
-            nc.scalar.copy(out=out_t[:, 0:HALF], in_=acc0[:])
-            nc.vector.tensor_copy(out=out_t[:, HALF:NB], in_=acc1[:])
-            out_sb = o_pool.tile([P, NT, O], F32)
+            nc.scalar.copy(out=out_t[:, 0:HALF], in_=acc[0][:])
+            nc.vector.tensor_copy(out=out_t[:, HALF:NB], in_=acc[1][:])
+            turned = []
             for h in range(NB // HALF):
                 ot = ot_psum.tile([P, 4, O], F32)
                 for q in range(4):
                     n = h * 4 + q
                     nc.tensor.transpose(ot[:, q, :], out_t[:, n * P : (n + 1) * P], ident_f[:])
-                if h == 0:
-                    nc.scalar.copy(out=out_sb[:, 0:4, :], in_=ot[:])
-                else:
-                    nc.vector.tensor_copy(out=out_sb[:, 4:8, :], in_=ot[:])
+                turned.append(ot)
+            return turned
+
+        def store(turned, c):
+            out_sb = o_pool.tile([P, NT, O], F32)
+            nc.scalar.copy(out=out_sb[:, 0:4, :], in_=turned[0][:])
+            nc.vector.tensor_copy(out=out_sb[:, 4:8, :], in_=turned[1][:])
             nc.sync.dma_start(out=out[c * NB : (c + 1) * NB, :].rearrange("(p n) o -> p n o", n=NT), in_=out_sb[:])
+
+        to_regroup = None
+        to_quantise = []
+        to_empty = None
+        to_store = None
+        t_next = t_first
+        xs_next = None
+        tp_wait = []
+
+        for step in range(NCH * NK + 4):
+            c, j = divmod(step, NK)
+            live = c < NCH
+            made = None
+            if live:
+                if j == 0:
+                    t = t_next
+                    acc0 = acc_psum.tile([P, HALF], F32)
+                    acc1 = acc_psum.tile([P, HALF], F32)
+                    acc = [acc0, acc1]
+                    lefts = {}
+                    s_prev = None
+                    if c + 1 < NCH:
+                        xs_next = load_x(c + 1)
+                s_cur = s_pool.tile([P, U, NB], F32)
+                sqs = []
+                for u in range(U):
+                    sq = sq_pool.tile([P, NB], F32)
+                    nc.scalar.activation(
+                        out=sq[:], in_=t[:, u, :], func=ACT.Square, bias=neg_g[:, u, j : j + 1], scale=1.0
+                    )
+                    sqs.append(sq)
+                for u in range(U):
+                    nc.vector.scalar_tensor_tensor(
+                        out=s_cur[:, u, :], in0=t[:, u, :], scalar=g[:, u, j : j + 1], in1=sqs[u][:],
+                        op0=ALU.subtract, op1=ALU.mult,
+                    )
+                if j >= 4:
+                    k = j - 4
+                    right = right_pool.tile([P, U, NB], BF16)
+                    inner = []
+                    for u in range(U):
+                        right_in = in_pool.tile([P, NB], F32)
+                        nc.scalar.activation(
+                            out=right_in[:], in_=s_prev[:, u, :], func=ACT.Relu, scale=e3[:, u, k : k + 1]
+                        )
+                        inner.append(right_in)
+                    for u in range(U):
+                        nc.vector.scalar_tensor_tensor(
+                            out=right[:, u, :], in0=s_cur[:, u, :], scalar=e4[:, u, k : k + 1], in1=inner[u][:],
+                            op0=ALU.mult, op1=ALU.subtract,
+                        )
+                if 1 <= j <= G:
+                    k = j - 1
+                    left = left_pool.tile([P, U, NB], BF16)
+                    lefts[k] = left
+                    inner = []
+                    for u in range(U):
+                        left_in = in_pool.tile([P, NB], F32)
+                        nc.scalar.activation(
+                            out=left_in[:], in_=s_cur[:, u, :], func=ACT.Relu, scale=c1[:, u, k : k + 1]
+                        )
+                        inner.append(left_in)
+                    for u in range(U):
+                        nc.vector.scalar_tensor_tensor(
+                            out=left[:, u, :], in0=s_prev[:, u, :], scalar=c0[:, u, k : k + 1], in1=inner[u][:],
+                            op0=ALU.mult, op1=ALU.subtract,
+                        )
+                if j == 4:
+                    base_grouped = grp_pool.tile([P, NB, U], BF16, tag="grp", align_bytes=64)
+                if j in (4, 5):
+                    lo = (j - 4) * HALF
+                    nc.scalar.activation(
+                        out=by_runs_dst(base_grouped, lo, lo + HALF), in_=by_runs_src(t, lo, lo + HALF), func=ACT.Silu
+                    )
+                if j >= 4:
+                    k = j - 4
+                    nc.vector.tensor_tensor(out=right[:], in0=lefts[k][:], in1=right[:], op=ALU.max)
+                    made = (right, k, acc, c)
+                s_prev = s_cur
+            if step == 0:
+                prepare_weights()
+
+            quantised = to_quantise
+            to_quantise = []
+            for grouped, plane, acc_of, c_of in quantised:
+                quantise_and_multiply(grouped, plane, acc_of)
+            if live and j == 5:
+                to_quantise.append((base_grouped, G, acc, c))
+            if to_regroup is not None:
+                plane_tile, plane, acc_of, c_of = to_regroup
+                to_quantise.append((regroup(plane_tile, SPLIT[j] if live else 352), plane, acc_of, c_of))
+            to_regroup = made
+            if to_store is not None:
+                store(to_store[0], to_store[1])
+                to_store = None
+            if to_empty is not None:
+                to_store = (empty_sums(to_empty[0]), to_empty[1])
+                to_empty = None
+            for grouped, plane, acc_of, c_of in quantised:
+                if plane == G - 1:
+                    to_empty = (acc_of, c_of)
+            if live and c + 1 < NCH:
+                if j == 8:
+                    t_next = t_pool.tile([P, U, NB], BF16, tag="t")
+                    tp_wait = [turn_x(xs_next, 0), turn_x(xs_next, 1)]
+                if j == 9:
+                    nc.scalar.copy(out=t_next[:, 0, :], in_=tp_wait[0][:])
+                    nc.scalar.copy(out=t_next[:, 1, :], in_=tp_wait[1][:])
+                    tp_wait = [turn_x(xs_next, 2), turn_x(xs_next, 3)]
+                if j == 10:
+                    nc.scalar.copy(out=t_next[:, 2, :], in_=tp_wait[0][:])
+                    nc.scalar.copy(out=t_next[:, 3, :], in_=tp_wait[1][:])

@@ -19,8 +19,9 @@ NT = NB // P
 NCH = B // NB
 NPL = G + 1
 HALF = 512
+GP_SHARE = 2
 RUN = 4
-SPLIT = {0:512,5:352,6:1024,7:864,8:864,9:704,10:704,11:864,12:864,13:864,14:864}
+SPLIT = {0:512,5:1024,6:1024,7:1024,8:1024,9:1024,10:1024,11:1024,12:800,13:800,14:512}
 
 FLOPS = 2 * B * I * O * NPL
 
@@ -38,11 +39,12 @@ def tile_kan_layer_t_kernel(tc, x, grid, coef, scale_base, scale_sp, mask, out):
         in_pool = ctx.enter_context(tc.tile_pool(name="inner", bufs=4))
         left_pool = ctx.enter_context(tc.tile_pool(name="left", bufs=4))
         right_pool = ctx.enter_context(tc.tile_pool(name="right", bufs=2))
-        grp_pool = ctx.enter_context(tc.tile_pool(name="grp", bufs=3))
+        grp_pool = ctx.enter_context(tc.tile_pool(name="grp", bufs=2))
+        base_pool = ctx.enter_context(tc.tile_pool(name="base", bufs=1))
         q_pool = ctx.enter_context(tc.tile_pool(name="q", bufs=2))
         o_pool = ctx.enter_context(tc.tile_pool(name="o", bufs=1))
-        tp_psum = ctx.enter_context(tc.psum_pool(name="tp", bufs=2))
-        acc_psum = ctx.enter_context(tc.psum_pool(name="acc", bufs=2))
+        tp_psum = ctx.enter_context(tc.psum_pool(name="tp", bufs=1))
+        acc_psum = ctx.enter_context(tc.psum_pool(name="acc", bufs=1))
         ot_psum = ctx.enter_context(tc.psum_pool(name="ot", bufs=2))
 
         ident_bf = const.tile([P, P], BF16)
@@ -59,7 +61,7 @@ def tile_kan_layer_t_kernel(tc, x, grid, coef, scale_base, scale_sp, mask, out):
             return xs
 
         def turn_x(xs, u):
-            tp = tp_psum.tile([P, NB], BF16)
+            tp = tp_psum.tile([P, NB], BF16, name="tp%d" % u)
             for n in range(NT):
                 nc.tensor.transpose(tp[:, n * P : (n + 1) * P], xs[:, n, u * P : (u + 1) * P], ident_bf[:])
             return tp
@@ -80,9 +82,10 @@ def tile_kan_layer_t_kernel(tc, x, grid, coef, scale_base, scale_sp, mask, out):
         nc.vector.tensor_scalar_mul(out=neg_g[:], in0=g[:], scalar1=-1.0)
 
         t_first = t_pool.tile([P, U, NB], BF16, tag="t")
+        tps_next = []
         for u in range(U):
-            tp0 = turn_x(xs0, u)
-            nc.scalar.copy(out=t_first[:, u, :], in_=tp0[:])
+            tps_next.append(turn_x(xs0, u))
+            nc.scalar.copy(out=t_first[:, u, :], in_=tps_next[u][:])
 
         d1 = const.tile([P, U, NK - 1], F32)
         nc.vector.tensor_sub(out=d1[:], in0=g[:, :, 1:NK], in1=g[:, :, 0 : NK - 1])
@@ -164,7 +167,7 @@ def tile_kan_layer_t_kernel(tc, x, grid, coef, scale_base, scale_sp, mask, out):
                     lhsT_scale=w_scales[:, w_cols],
                     rhs=codes[:, cols].bitcast(FP8X4),
                     rhs_scale=scales[:, cols],
-                    start=(plane == G),
+                    start=(plane == 0),
                     stop=(plane == G - 1),
                 )
 
@@ -205,7 +208,6 @@ def tile_kan_layer_t_kernel(tc, x, grid, coef, scale_base, scale_sp, mask, out):
         to_store = None
         t_next = t_first
         xs_next = None
-        tp_wait = []
 
         for step in range(NCH * NK + 4):
             c, j = divmod(step, NK)
@@ -214,9 +216,7 @@ def tile_kan_layer_t_kernel(tc, x, grid, coef, scale_base, scale_sp, mask, out):
             if live:
                 if j == 0:
                     t = t_next
-                    acc0 = acc_psum.tile([P, HALF], F32)
-                    acc1 = acc_psum.tile([P, HALF], F32)
-                    acc = [acc0, acc1]
+                    tps = tps_next
                     lefts = {}
                     s_prev = None
                     if c + 1 < NCH:
@@ -231,9 +231,25 @@ def tile_kan_layer_t_kernel(tc, x, grid, coef, scale_base, scale_sp, mask, out):
                     sqs.append(sq)
                 for u in range(U):
                     nc.vector.scalar_tensor_tensor(
-                        out=s_cur[:, u, :], in0=t[:, u, :], scalar=g[:, u, j : j + 1], in1=sqs[u][:],
+                        out=s_cur[:, u, :], in0=tps[u][:], scalar=g[:, u, j : j + 1], in1=sqs[u][:],
                         op0=ALU.subtract, op1=ALU.mult,
                     )
+                if j == NK - 1 and c + 1 < NCH:
+                    tps_next = [turn_x(xs_next, u) for u in range(U)]
+                if 1 <= j <= G:
+                    k = j - 1
+                    inner_left = []
+                    for u in range(GP_SHARE):
+                        left_gp = in_pool.tile([P, NB], F32, bufs=2)
+                        nc.gpsimd.tensor_scalar(
+                            out=left_gp[:], in0=s_cur[:, u, :], scalar1=c1[:, u, k : k + 1], scalar2=0.0,
+                            op0=ALU.mult, op1=ALU.max,
+                        )
+                        inner_left.append(left_gp)
+                if j == 4:
+                    acc0 = acc_psum.tile([P, HALF], F32)
+                    acc1 = acc_psum.tile([P, HALF], F32)
+                    acc = [acc0, acc1]
                 if j >= 4:
                     k = j - 4
                     right = right_pool.tile([P, U, NB], BF16)
@@ -253,24 +269,23 @@ def tile_kan_layer_t_kernel(tc, x, grid, coef, scale_base, scale_sp, mask, out):
                     k = j - 1
                     left = left_pool.tile([P, U, NB], BF16)
                     lefts[k] = left
-                    inner = []
-                    for u in range(U):
-                        left_in = in_pool.tile([P, NB], F32)
+                    for u in range(GP_SHARE, U):
+                        left_in = in_pool.tile([P, NB], F32, bufs=3)
                         nc.scalar.activation(
                             out=left_in[:], in_=s_cur[:, u, :], func=ACT.Relu, scale=c1[:, u, k : k + 1]
                         )
-                        inner.append(left_in)
+                        inner_left.append(left_in)
                     for u in range(U):
                         nc.vector.scalar_tensor_tensor(
-                            out=left[:, u, :], in0=s_prev[:, u, :], scalar=c0[:, u, k : k + 1], in1=inner[u][:],
+                            out=left[:, u, :], in0=s_prev[:, u, :], scalar=c0[:, u, k : k + 1], in1=inner_left[u][:],
                             op0=ALU.mult, op1=ALU.subtract,
                         )
-                if j == 4:
-                    base_grouped = grp_pool.tile([P, NB, U], BF16, tag="grp", align_bytes=64)
-                if j in (4, 5):
-                    lo = (j - 4) * HALF
+                if j == 7:
+                    base_grouped = base_pool.tile([P, NB, U], BF16, align_bytes=64)
+                if 7 <= j <= 10:
+                    lo = (j - 7) * (NB // 4)
                     nc.scalar.activation(
-                        out=by_runs_dst(base_grouped, lo, lo + HALF), in_=by_runs_src(t, lo, lo + HALF), func=ACT.Silu
+                        out=by_runs_dst(base_grouped, lo, lo + NB // 4), in_=by_runs_src(t, lo, lo + NB // 4), func=ACT.Silu
                     )
                 if j >= 4:
                     k = j - 4
@@ -284,7 +299,7 @@ def tile_kan_layer_t_kernel(tc, x, grid, coef, scale_base, scale_sp, mask, out):
             to_quantise = []
             for grouped, plane, acc_of, c_of in quantised:
                 quantise_and_multiply(grouped, plane, acc_of)
-            if live and j == 5:
+            if live and j == 10:
                 to_quantise.append((base_grouped, G, acc, c))
             if to_regroup is not None:
                 plane_tile, plane, acc_of, c_of = to_regroup
@@ -299,14 +314,7 @@ def tile_kan_layer_t_kernel(tc, x, grid, coef, scale_base, scale_sp, mask, out):
             for grouped, plane, acc_of, c_of in quantised:
                 if plane == G - 1:
                     to_empty = (acc_of, c_of)
-            if live and c + 1 < NCH:
-                if j == 8:
-                    t_next = t_pool.tile([P, U, NB], BF16, tag="t")
-                    tp_wait = [turn_x(xs_next, 0), turn_x(xs_next, 1)]
-                if j == 9:
-                    nc.scalar.copy(out=t_next[:, 0, :], in_=tp_wait[0][:])
-                    nc.scalar.copy(out=t_next[:, 1, :], in_=tp_wait[1][:])
-                    tp_wait = [turn_x(xs_next, 2), turn_x(xs_next, 3)]
-                if j == 10:
-                    nc.scalar.copy(out=t_next[:, 2, :], in_=tp_wait[0][:])
-                    nc.scalar.copy(out=t_next[:, 3, :], in_=tp_wait[1][:])
+            if live and c + 1 < NCH and j == NK - 1:
+                t_next = t_pool.tile([P, U, NB], BF16, tag="t")
+                for u in range(U):
+                    nc.scalar.copy(out=t_next[:, u, :], in_=tps_next[u][:])

@@ -19,9 +19,9 @@ NT = NB // P
 NCH = B // NB
 NPL = G + 1
 HALF = 512
-GP_SHARE = 2
+GPC = 768
 RUN = 4
-SPLIT = {0:512,5:1024,6:1024,7:1024,8:1024,9:1024,10:1024,11:1024,12:800,13:800,14:512}
+SPLIT = {0:512,5:384,6:576,7:576,8:896,9:736,10:736,11:736,12:864,13:864,14:512}
 
 FLOPS = 2 * B * I * O * NPL
 
@@ -33,7 +33,7 @@ def tile_kan_layer_t_kernel(tc, x, grid, coef, scale_base, scale_sp, mask, out):
         const = ctx.enter_context(tc.tile_pool(name="const", bufs=1))
         wprep = ctx.enter_context(tc.tile_pool(name="wprep", bufs=1))
         xs_pool = ctx.enter_context(tc.tile_pool(name="xs", bufs=1))
-        t_pool = ctx.enter_context(tc.tile_pool(name="t", bufs=2))
+        t_pool = ctx.enter_context(tc.tile_pool(name="t", bufs=1))
         s_pool = ctx.enter_context(tc.tile_pool(name="s", bufs=2))
         sq_pool = ctx.enter_context(tc.tile_pool(name="sq", bufs=4))
         in_pool = ctx.enter_context(tc.tile_pool(name="inner", bufs=4))
@@ -218,6 +218,8 @@ def tile_kan_layer_t_kernel(tc, x, grid, coef, scale_base, scale_sp, mask, out):
                     t = t_next
                     tps = tps_next
                     lefts = {}
+                    scaled = {}
+                    held = {}
                     s_prev = None
                     if c + 1 < NCH:
                         xs_next = load_x(c + 1)
@@ -236,16 +238,18 @@ def tile_kan_layer_t_kernel(tc, x, grid, coef, scale_base, scale_sp, mask, out):
                     )
                 if j == NK - 1 and c + 1 < NCH:
                     tps_next = [turn_x(xs_next, u) for u in range(U)]
-                if 1 <= j <= G:
-                    k = j - 1
-                    inner_left = []
-                    for u in range(GP_SHARE):
-                        left_gp = in_pool.tile([P, NB], F32, bufs=2)
-                        nc.gpsimd.tensor_scalar(
-                            out=left_gp[:], in0=s_cur[:, u, :], scalar1=c1[:, u, k : k + 1], scalar2=0.0,
-                            op0=ALU.mult, op1=ALU.max,
-                        )
-                        inner_left.append(left_gp)
+                if j < G:
+                    a_gp = in_pool.tile([P, GPC], F32, bufs=3)
+                    nc.gpsimd.tensor_scalar(
+                        out=a_gp[:], in0=s_cur[:, 0, 0:GPC], scalar1=c0[:, 0, j : j + 1], scalar2=0.0,
+                        op0=ALU.mult, op1=ALU.add,
+                    )
+                    scaled[j] = a_gp
+                if 2 <= j <= G + 1:
+                    k = j - 2
+                    nc.gpsimd.tensor_tensor(
+                        out=lefts[k][:, 0, 0:GPC], in0=scaled[k][:], in1=held[k][:, 0:GPC], op=ALU.subtract
+                    )
                 if j == 4:
                     acc0 = acc_psum.tile([P, HALF], F32)
                     acc1 = acc_psum.tile([P, HALF], F32)
@@ -269,21 +273,28 @@ def tile_kan_layer_t_kernel(tc, x, grid, coef, scale_base, scale_sp, mask, out):
                     k = j - 1
                     left = left_pool.tile([P, U, NB], BF16)
                     lefts[k] = left
-                    for u in range(GP_SHARE, U):
+                    left_held = in_pool.tile([P, NB], F32, bufs=2)
+                    nc.scalar.activation(
+                        out=left_held[:], in_=s_cur[:, 0, :], func=ACT.Relu, scale=c1[:, 0, k : k + 1]
+                    )
+                    held[k] = left_held
+                    inner = [left_held]
+                    for u in range(1, U):
                         left_in = in_pool.tile([P, NB], F32, bufs=3)
                         nc.scalar.activation(
                             out=left_in[:], in_=s_cur[:, u, :], func=ACT.Relu, scale=c1[:, u, k : k + 1]
                         )
-                        inner_left.append(left_in)
+                        inner.append(left_in)
                     for u in range(U):
+                        lo = GPC if u == 0 else 0
                         nc.vector.scalar_tensor_tensor(
-                            out=left[:, u, :], in0=s_prev[:, u, :], scalar=c0[:, u, k : k + 1], in1=inner_left[u][:],
+                            out=left[:, u, lo:NB], in0=s_prev[:, u, lo:NB], scalar=c0[:, u, k : k + 1], in1=inner[u][:, lo:NB],
                             op0=ALU.mult, op1=ALU.subtract,
                         )
-                if j == 7:
+                if j == 4:
                     base_grouped = base_pool.tile([P, NB, U], BF16, align_bytes=64)
-                if 7 <= j <= 10:
-                    lo = (j - 7) * (NB // 4)
+                if 4 <= j <= 7:
+                    lo = (j - 4) * (NB // 4)
                     nc.scalar.activation(
                         out=by_runs_dst(base_grouped, lo, lo + NB // 4), in_=by_runs_src(t, lo, lo + NB // 4), func=ACT.Silu
                     )
@@ -299,7 +310,7 @@ def tile_kan_layer_t_kernel(tc, x, grid, coef, scale_base, scale_sp, mask, out):
             to_quantise = []
             for grouped, plane, acc_of, c_of in quantised:
                 quantise_and_multiply(grouped, plane, acc_of)
-            if live and j == 10:
+            if live and j == 7:
                 to_quantise.append((base_grouped, G, acc, c))
             if to_regroup is not None:
                 plane_tile, plane, acc_of, c_of = to_regroup

@@ -19,9 +19,10 @@ NT = NB // P
 NCH = B // NB
 NPL = G + 1
 HALF = 512
-GPC = 768
+GPY = 768
+Y_STEPS = (13, 14)
 RUN = 4
-SPLIT = {0:512,5:384,6:576,7:576,8:896,9:736,10:736,11:736,12:864,13:864,14:512}
+SPLIT = {0:512,5:352,6:544,7:544,8:864,9:704,10:704,11:704,12:864,13:736,14:384}
 
 FLOPS = 2 * B * I * O * NPL
 
@@ -116,6 +117,8 @@ def tile_kan_layer_t_kernel(tc, x, grid, coef, scale_base, scale_sp, mask, out):
         nc.vector.tensor_mul(out=e3[:], in0=e3[:], in1=d4[:])
         nc.vector.tensor_scalar_mul(out=e3[:], in0=e3[:], scalar1=-1.0)
 
+        zero = const.tile([P, 1], F32)
+        gate_out = const.tile([P, 1], F32)
         w_codes = const.tile([P, NPL * O], U32, align_bytes=64)
         w_scales = const.tile([P, NPL * O], U8, align_bytes=64)
 
@@ -231,6 +234,8 @@ def tile_kan_layer_t_kernel(tc, x, grid, coef, scale_base, scale_sp, mask, out):
                         out=sq[:], in_=t[:, u, :], func=ACT.Square, bias=neg_g[:, u, j : j + 1], scale=1.0
                     )
                     sqs.append(sq)
+                if 1 <= j <= G + 1:
+                    nc.vector.memset(zero[:], 0.0)
                 for u in range(U):
                     nc.vector.scalar_tensor_tensor(
                         out=s_cur[:, u, :], in0=tps[u][:], scalar=g[:, u, j : j + 1], in1=sqs[u][:],
@@ -238,18 +243,21 @@ def tile_kan_layer_t_kernel(tc, x, grid, coef, scale_base, scale_sp, mask, out):
                     )
                 if j == NK - 1 and c + 1 < NCH:
                     tps_next = [turn_x(xs_next, u) for u in range(U)]
-                if j < G:
-                    a_gp = in_pool.tile([P, GPC], F32, bufs=3)
+                if 1 <= j <= G:
+                    k = j - 1
+                    a_gp = in_pool.tile([P, NB], F32, bufs=2)
                     nc.gpsimd.tensor_scalar(
-                        out=a_gp[:], in0=s_cur[:, 0, 0:GPC], scalar1=c0[:, 0, j : j + 1], scalar2=0.0,
+                        out=a_gp[:], in0=s_prev[:, 0, :], scalar1=c0[:, 0, k : k + 1], scalar2=zero[:, 0:1],
                         op0=ALU.mult, op1=ALU.add,
                     )
-                    scaled[j] = a_gp
+                    scaled[k] = a_gp
+                if j == G + 1:
+                    nc.gpsimd.tensor_scalar(
+                        out=gate_out[:], in0=zero[:], scalar1=1.0, scalar2=0.0, op0=ALU.mult, op1=ALU.add
+                    )
                 if 2 <= j <= G + 1:
                     k = j - 2
-                    nc.gpsimd.tensor_tensor(
-                        out=lefts[k][:, 0, 0:GPC], in0=scaled[k][:], in1=held[k][:, 0:GPC], op=ALU.subtract
-                    )
+                    nc.gpsimd.tensor_tensor(out=lefts[k][:, 0, :], in0=scaled[k][:], in1=held[k][:], op=ALU.subtract)
                 if j == 4:
                     acc0 = acc_psum.tile([P, HALF], F32)
                     acc1 = acc_psum.tile([P, HALF], F32)
@@ -264,9 +272,19 @@ def tile_kan_layer_t_kernel(tc, x, grid, coef, scale_base, scale_sp, mask, out):
                             out=right_in[:], in_=s_prev[:, u, :], func=ACT.Relu, scale=e3[:, u, k : k + 1]
                         )
                         inner.append(right_in)
+                    if j in Y_STEPS:
+                        a_gp = in_pool.tile([P, NB], F32, bufs=2)
+                        nc.gpsimd.tensor_scalar(
+                            out=a_gp[:, 0:GPY], in0=s_cur[:, 0, 0:GPY], scalar1=e4[:, 0, k : k + 1], scalar2=0.0,
+                            op0=ALU.mult, op1=ALU.add,
+                        )
+                        nc.gpsimd.tensor_tensor(
+                            out=right[:, 0, 0:GPY], in0=a_gp[:, 0:GPY], in1=inner[0][:, 0:GPY], op=ALU.subtract
+                        )
                     for u in range(U):
+                        lo = GPY if (u == 0 and j in Y_STEPS) else 0
                         nc.vector.scalar_tensor_tensor(
-                            out=right[:, u, :], in0=s_cur[:, u, :], scalar=e4[:, u, k : k + 1], in1=inner[u][:],
+                            out=right[:, u, lo:NB], in0=s_cur[:, u, lo:NB], scalar=e4[:, u, k : k + 1], in1=inner[u][:, lo:NB],
                             op0=ALU.mult, op1=ALU.subtract,
                         )
                 if 1 <= j <= G:
@@ -285,10 +303,9 @@ def tile_kan_layer_t_kernel(tc, x, grid, coef, scale_base, scale_sp, mask, out):
                             out=left_in[:], in_=s_cur[:, u, :], func=ACT.Relu, scale=c1[:, u, k : k + 1]
                         )
                         inner.append(left_in)
-                    for u in range(U):
-                        lo = GPC if u == 0 else 0
+                    for u in range(1, U):
                         nc.vector.scalar_tensor_tensor(
-                            out=left[:, u, lo:NB], in0=s_prev[:, u, lo:NB], scalar=c0[:, u, k : k + 1], in1=inner[u][:, lo:NB],
+                            out=left[:, u, :], in0=s_prev[:, u, :], scalar=c0[:, u, k : k + 1], in1=inner[u][:],
                             op0=ALU.mult, op1=ALU.subtract,
                         )
                 if j == 4:

@@ -22,7 +22,7 @@ HALF = 512
 GPY = 768
 Y_STEPS = (13, 14)
 RUN = 4
-SPLIT = {0:512,5:352,6:544,7:544,8:864,9:704,10:704,11:704,12:864,13:736,14:384}
+SPLIT = {0:448,5:288,6:480,7:480,8:800,9:640,10:640,11:640,12:800,13:672,14:320}
 
 FLOPS = 2 * B * I * O * NPL
 

@@ -20,9 +20,10 @@ NCH = B // NB
 NPL = G + 1
 HALF = 512
 GPY = 768
+GPX1 = 608
 Y_STEPS = (13, 14)
 RUN = 4
-SPLIT = {0:448,5:288,6:480,7:480,8:800,9:640,10:640,11:640,12:800,13:672,14:320}
+SPLIT = {0:480,5:224,6:416,7:416,8:736,9:576,10:576,11:576,12:832,13:704,14:352}
 
 FLOPS = 2 * B * I * O * NPL
 
@@ -82,11 +83,6 @@ def tile_kan_layer_t_kernel(tc, x, grid, coef, scale_base, scale_sp, mask, out):
         neg_g = const.tile([P, U, NK], F32)
         nc.vector.tensor_scalar_mul(out=neg_g[:], in0=g[:], scalar1=-1.0)
 
-        t_first = t_pool.tile([P, U, NB], BF16, tag="t")
-        tps_next = []
-        for u in range(U):
-            tps_next.append(turn_x(xs0, u))
-            nc.scalar.copy(out=t_first[:, u, :], in_=tps_next[u][:])
 
         d1 = const.tile([P, U, NK - 1], F32)
         nc.vector.tensor_sub(out=d1[:], in0=g[:, :, 1:NK], in1=g[:, :, 0 : NK - 1])
@@ -106,6 +102,15 @@ def tile_kan_layer_t_kernel(tc, x, grid, coef, scale_base, scale_sp, mask, out):
 
         c0 = product("c0", [d1[:, :, 0:G], d2[:, :, 0:G], d3[:, :, 0:G]])
         nc.vector.reciprocal(out=c0[:], in_=c0[:])
+        kap = const.tile([P, U, G], F32)
+        nc.scalar.activation(out=kap[:], in_=c0[:], func=ACT.Sqrt)
+        ksq = const.tile([P, U, NK], F32)
+        nc.vector.memset(ksq[:], 1.0)
+        t_first = t_pool.tile([P, U, NB], BF16, tag="t")
+        tps_next = []
+        for u in range(U):
+            tps_next.append(turn_x(xs0, u))
+            nc.scalar.copy(out=t_first[:, u, :], in_=tps_next[u][:])
         c1 = product("c1", [d1[:, :, 0:G], d1[:, :, 1 : G + 1], d2[:, :, 1 : G + 1], d3[:, :, 1 : G + 1]])
         nc.vector.reciprocal(out=c1[:], in_=c1[:])
         nc.vector.tensor_mul(out=c1[:], in0=c1[:], in1=d4[:])
@@ -116,6 +121,19 @@ def tile_kan_layer_t_kernel(tc, x, grid, coef, scale_base, scale_sp, mask, out):
         nc.vector.reciprocal(out=e3[:], in_=e3[:])
         nc.vector.tensor_mul(out=e3[:], in0=e3[:], in1=d4[:])
         nc.vector.tensor_scalar_mul(out=e3[:], in0=e3[:], scalar1=-1.0)
+        rk = const.tile([P, U, G], F32)
+        nc.vector.reciprocal(out=rk[:], in_=kap[:])
+        nc.vector.tensor_mul(out=rk[:], in0=rk[:], in1=c0[:])
+        nc.vector.tensor_add(out=rk[:], in0=rk[:], in1=kap[:])
+        nc.vector.tensor_scalar_mul(out=ksq[:, :, 0:G], in0=rk[:], scalar1=0.5)
+        nb = const.tile([P, U, NK], F32)
+        nc.vector.tensor_mul(out=nb[:], in0=ksq[:], in1=neg_g[:])
+        k2 = const.tile([P, U, NK], F32)
+        nc.vector.tensor_mul(out=k2[:], in0=ksq[:], in1=ksq[:])
+        nc.vector.reciprocal(out=k2[:], in_=k2[:])
+        nc.vector.tensor_mul(out=c1[:], in0=c1[:], in1=k2[:, :, 1 : G + 1])
+        nc.vector.tensor_mul(out=e3[:], in0=e3[:], in1=k2[:, :, 3 : G + 3])
+        nc.vector.tensor_mul(out=e4[:], in0=e4[:], in1=k2[:, :, 4 : G + 4])
 
         zero = const.tile([P, 1], F32)
         gate_out = const.tile([P, 1], F32)
@@ -221,43 +239,39 @@ def tile_kan_layer_t_kernel(tc, x, grid, coef, scale_base, scale_sp, mask, out):
                     t = t_next
                     tps = tps_next
                     lefts = {}
-                    scaled = {}
                     held = {}
                     s_prev = None
+                    s_older = None
                     if c + 1 < NCH:
                         xs_next = load_x(c + 1)
-                s_cur = s_pool.tile([P, U, NB], F32)
+                s01 = s_pool.tile([P, 2, NB], F32, bufs=3)
+                s23 = s_pool.tile([P, 2, NB], F32, bufs=2)
+                s_cur = [s01[:, 0, :], s01[:, 1, :], s23[:, 0, :], s23[:, 1, :]]
                 sqs = []
                 for u in range(U):
                     sq = sq_pool.tile([P, NB], F32)
                     nc.scalar.activation(
-                        out=sq[:], in_=t[:, u, :], func=ACT.Square, bias=neg_g[:, u, j : j + 1], scale=1.0
+                        out=sq[:], in_=t[:, u, :], func=ACT.Square, bias=nb[:, u, j : j + 1], scale=ksq[:, u, j : j + 1]
                     )
                     sqs.append(sq)
-                if 1 <= j <= G + 1:
+                if 2 <= j <= G + 1:
                     nc.vector.memset(zero[:], 0.0)
                 for u in range(U):
                     nc.vector.scalar_tensor_tensor(
-                        out=s_cur[:, u, :], in0=tps[u][:], scalar=g[:, u, j : j + 1], in1=sqs[u][:],
+                        out=s_cur[u], in0=tps[u][:], scalar=g[:, u, j : j + 1], in1=sqs[u][:],
                         op0=ALU.subtract, op1=ALU.mult,
                     )
                 if j == NK - 1 and c + 1 < NCH:
                     tps_next = [turn_x(xs_next, u) for u in range(U)]
-                if 1 <= j <= G:
-                    k = j - 1
-                    a_gp = in_pool.tile([P, NB], F32, bufs=2)
-                    nc.gpsimd.tensor_scalar(
-                        out=a_gp[:], in0=s_prev[:, 0, :], scalar1=c0[:, 0, k : k + 1], scalar2=zero[:, 0:1],
-                        op0=ALU.mult, op1=ALU.add,
-                    )
-                    scaled[k] = a_gp
-                if j == G + 1:
+                if 2 <= j <= G + 1:
+                    k = j - 2
                     nc.gpsimd.tensor_scalar(
                         out=gate_out[:], in0=zero[:], scalar1=1.0, scalar2=0.0, op0=ALU.mult, op1=ALU.add
                     )
-                if 2 <= j <= G + 1:
-                    k = j - 2
-                    nc.gpsimd.tensor_tensor(out=lefts[k][:, 0, :], in0=scaled[k][:], in1=held[k][:], op=ALU.subtract)
+                    nc.gpsimd.tensor_tensor(out=lefts[k][:, 0, :], in0=s_older[0], in1=held[k][0][:], op=ALU.subtract)
+                    nc.gpsimd.tensor_tensor(
+                        out=lefts[k][:, 1, 0:GPX1], in0=s_older[1][:, 0:GPX1], in1=held[k][1][:, 0:GPX1], op=ALU.subtract
+                    )
                 if j == 4:
                     acc0 = acc_psum.tile([P, HALF], F32)
                     acc1 = acc_psum.tile([P, HALF], F32)
@@ -267,15 +281,15 @@ def tile_kan_layer_t_kernel(tc, x, grid, coef, scale_base, scale_sp, mask, out):
                     right = right_pool.tile([P, U, NB], BF16)
                     inner = []
                     for u in range(U):
-                        right_in = in_pool.tile([P, NB], F32)
+                        right_in = in_pool.tile([P, NB], F32, bufs=4)
                         nc.scalar.activation(
-                            out=right_in[:], in_=s_prev[:, u, :], func=ACT.Relu, scale=e3[:, u, k : k + 1]
+                            out=right_in[:], in_=s_prev[u], func=ACT.Relu, scale=e3[:, u, k : k + 1]
                         )
                         inner.append(right_in)
                     if j in Y_STEPS:
-                        a_gp = in_pool.tile([P, NB], F32, bufs=2)
+                        a_gp = in_pool.tile([P, NB], F32, bufs=1)
                         nc.gpsimd.tensor_scalar(
-                            out=a_gp[:, 0:GPY], in0=s_cur[:, 0, 0:GPY], scalar1=e4[:, 0, k : k + 1], scalar2=0.0,
+                            out=a_gp[:, 0:GPY], in0=s_cur[0][:, 0:GPY], scalar1=e4[:, 0, k : k + 1], scalar2=0.0,
                             op0=ALU.mult, op1=ALU.add,
                         )
                         nc.gpsimd.tensor_tensor(
@@ -284,29 +298,28 @@ def tile_kan_layer_t_kernel(tc, x, grid, coef, scale_base, scale_sp, mask, out):
                     for u in range(U):
                         lo = GPY if (u == 0 and j in Y_STEPS) else 0
                         nc.vector.scalar_tensor_tensor(
-                            out=right[:, u, lo:NB], in0=s_cur[:, u, lo:NB], scalar=e4[:, u, k : k + 1], in1=inner[u][:, lo:NB],
+                            out=right[:, u, lo:NB], in0=s_cur[u][:, lo:NB], scalar=e4[:, u, k : k + 1], in1=inner[u][:, lo:NB],
                             op0=ALU.mult, op1=ALU.subtract,
                         )
                 if 1 <= j <= G:
                     k = j - 1
                     left = left_pool.tile([P, U, NB], BF16)
                     lefts[k] = left
-                    left_held = in_pool.tile([P, NB], F32, bufs=2)
-                    nc.scalar.activation(
-                        out=left_held[:], in_=s_cur[:, 0, :], func=ACT.Relu, scale=c1[:, 0, k : k + 1]
-                    )
-                    held[k] = left_held
-                    inner = [left_held]
-                    for u in range(1, U):
-                        left_in = in_pool.tile([P, NB], F32, bufs=3)
-                        nc.scalar.activation(
-                            out=left_in[:], in_=s_cur[:, u, :], func=ACT.Relu, scale=c1[:, u, k : k + 1]
-                        )
+                    left_held0 = in_pool.tile([P, NB], F32, bufs=2)
+                    left_held1 = in_pool.tile([P, NB], F32, bufs=2)
+                    inner = [left_held0, left_held1]
+                    held[k] = inner
+                    for u in range(2, U):
+                        left_in = in_pool.tile([P, NB], F32, bufs=2)
                         inner.append(left_in)
+                    for u in (1, 2, 3, 0):
+                        nc.scalar.activation(
+                            out=inner[u][:], in_=s_cur[u], func=ACT.Relu, scale=c1[:, u, k : k + 1]
+                        )
                     for u in range(1, U):
-                        nc.vector.scalar_tensor_tensor(
-                            out=left[:, u, :], in0=s_prev[:, u, :], scalar=c0[:, u, k : k + 1], in1=inner[u][:],
-                            op0=ALU.mult, op1=ALU.subtract,
+                        lo = GPX1 if u == 1 else 0
+                        nc.vector.tensor_tensor(
+                            out=left[:, u, lo:NB], in0=s_prev[u][:, lo:NB], in1=inner[u][:, lo:NB], op=ALU.subtract
                         )
                 if j == 4:
                     base_grouped = base_pool.tile([P, NB, U], BF16, align_bytes=64)
@@ -319,6 +332,7 @@ def tile_kan_layer_t_kernel(tc, x, grid, coef, scale_base, scale_sp, mask, out):
                     k = j - 4
                     nc.vector.tensor_tensor(out=right[:], in0=lefts[k][:], in1=right[:], op=ALU.max)
                     made = (right, k, acc, c)
+                s_older = s_prev
                 s_prev = s_cur
             if step == 0:
                 prepare_weights()

@@ -19,11 +19,11 @@ NT = NB // P
 NCH = B // NB
 NPL = G + 1
 HALF = 512
-GPY = 768
-GPX1 = 608
-Y_STEPS = (13, 14)
+GX = 2048
+LV = 2
+LJ = 3
 RUN = 4
-SPLIT = {0:480,5:224,6:416,7:416,8:736,9:576,10:576,11:576,12:832,13:704,14:352}
+BUSY, IDLE = 512, 768
 
 FLOPS = 2 * B * I * O * NPL
 
@@ -36,10 +36,10 @@ def tile_kan_layer_t_kernel(tc, x, grid, coef, scale_base, scale_sp, mask, out):
         wprep = ctx.enter_context(tc.tile_pool(name="wprep", bufs=1))
         xs_pool = ctx.enter_context(tc.tile_pool(name="xs", bufs=1))
         t_pool = ctx.enter_context(tc.tile_pool(name="t", bufs=1))
-        s_pool = ctx.enter_context(tc.tile_pool(name="s", bufs=2))
+        s_pool = ctx.enter_context(tc.tile_pool(name="s", bufs=3))
         sq_pool = ctx.enter_context(tc.tile_pool(name="sq", bufs=4))
-        in_pool = ctx.enter_context(tc.tile_pool(name="inner", bufs=4))
-        left_pool = ctx.enter_context(tc.tile_pool(name="left", bufs=4))
+        in_pool = ctx.enter_context(tc.tile_pool(name="inner", bufs=1))
+        left_pool = ctx.enter_context(tc.tile_pool(name="left", bufs=3))
         right_pool = ctx.enter_context(tc.tile_pool(name="right", bufs=2))
         grp_pool = ctx.enter_context(tc.tile_pool(name="grp", bufs=2))
         base_pool = ctx.enter_context(tc.tile_pool(name="base", bufs=1))
@@ -142,7 +142,7 @@ def tile_kan_layer_t_kernel(tc, x, grid, coef, scale_base, scale_sp, mask, out):
 
         def prepare_weights():
             msp = wprep.tile([P, U, O], F32)
-            nc.vector.tensor_mul(out=msp[:], in0=mask_sb[:], in1=sp_sb[:])
+            nc.gpsimd.tensor_mul(out=msp[:], in0=mask_sb[:], in1=sp_sb[:])
             coef_v = coef_sb[:].rearrange("p u (o k) -> p k o u", k=G)
             for first, count in ((0, 8), (8, 4)):
                 w_grouped = grp_pool.tile([P, NB, U], BF16, tag="grp", align_bytes=64)
@@ -151,11 +151,11 @@ def tile_kan_layer_t_kernel(tc, x, grid, coef, scale_base, scale_sp, mask, out):
                     plane = first + n
                     dst = w_flat[:, n * O * U : (n + 1) * O * U].rearrange("p (o u) -> p o u", u=U)
                     if plane < G:
-                        nc.vector.tensor_tensor(
+                        nc.gpsimd.tensor_tensor(
                             out=dst, in0=coef_v[:, plane, :, :], in1=msp[:].rearrange("p u o -> p o u"), op=ALU.mult
                         )
                     else:
-                        nc.vector.tensor_tensor(
+                        nc.gpsimd.tensor_tensor(
                             out=dst,
                             in0=mask_sb[:].rearrange("p u o -> p o u"),
                             in1=base_sb[:].rearrange("p u o -> p o u"),
@@ -192,15 +192,15 @@ def tile_kan_layer_t_kernel(tc, x, grid, coef, scale_base, scale_sp, mask, out):
                     stop=(plane == G - 1),
                 )
 
-        def regroup(plane_tile, split):
+        def regroup(plane_tile, sc):
             grouped = grp_pool.tile([P, NB, U], BF16, tag="grp", align_bytes=64)
-            if split > 0:
+            if sc > 0:
                 nc.scalar.activation(
-                    out=by_runs_dst(grouped, 0, split), in_=by_runs_src(plane_tile, 0, split), func=ACT.Relu
+                    out=by_runs_dst(grouped, 0, sc), in_=by_runs_src(plane_tile, 0, sc), func=ACT.Relu
                 )
-            if split < NB:
+            if sc < NB:
                 nc.vector.tensor_scalar_max(
-                    out=by_runs_dst(grouped, split, NB), in0=by_runs_src(plane_tile, split, NB), scalar1=0.0
+                    out=by_runs_dst(grouped, sc, NB), in0=by_runs_src(plane_tile, sc, NB), scalar1=0.0
                 )
             return grouped
 
@@ -223,117 +223,77 @@ def tile_kan_layer_t_kernel(tc, x, grid, coef, scale_base, scale_sp, mask, out):
             nc.vector.tensor_copy(out=out_sb[:, 4:8, :], in_=turned[1][:])
             nc.sync.dma_start(out=out[c * NB : (c + 1) * NB, :].rearrange("(p n) o -> p n o", n=NT), in_=out_sb[:])
 
+        def squares(t, j):
+            sqs = []
+            for u in range(U):
+                sq = sq_pool.tile([P, NB], F32)
+                nc.scalar.activation(
+                    out=sq[:], in_=t[:, u, :], func=ACT.Square, bias=nb[:, u, j : j + 1], scale=ksq[:, u, j : j + 1]
+                )
+                sqs.append(sq)
+            return sqs
+
+        def flat(tile, lo, hi):
+            return tile[:].rearrange("p u b -> p (u b)")[:, lo:hi]
+
+        to_left = None
         to_regroup = None
         to_quantise = []
         to_empty = None
         to_store = None
-        t_next = t_first
-        xs_next = None
+        t = t_first
+        tps = tps_next
+        sqs = squares(t, 0)
+        s_prev = None
+        right_in = None
+        lefts = {}
 
         for step in range(NCH * NK + 4):
             c, j = divmod(step, NK)
             live = c < NCH
             made = None
+            left_job = to_left
+            to_left = None
+            if live and j == 4:
+                acc0 = acc_psum.tile([P, HALF], F32)
+                acc1 = acc_psum.tile([P, HALF], F32)
+                acc = [acc0, acc1]
+            if live and j == 0 and c + 1 < NCH:
+                xs_next = load_x(c + 1)
+
+            if left_job is not None:
+                s_first, left_in, left = left_job
+                nc.vector.memset(zero[:], 0.0)
+                nc.gpsimd.tensor_scalar(
+                    out=gate_out[:], in0=zero[:], scalar1=1.0, scalar2=0.0, op0=ALU.mult, op1=ALU.add
+                )
+                nc.gpsimd.tensor_tensor(
+                    out=flat(left, 0, GX), in0=flat(s_first, 0, GX), in1=flat(left_in, 0, GX), op=ALU.subtract
+                )
             if live:
-                if j == 0:
-                    t = t_next
-                    tps = tps_next
-                    lefts = {}
-                    held = {}
-                    s_prev = None
-                    s_older = None
-                    if c + 1 < NCH:
-                        xs_next = load_x(c + 1)
-                s01 = s_pool.tile([P, 2, NB], F32, bufs=3)
-                s23 = s_pool.tile([P, 2, NB], F32, bufs=2)
-                s_cur = [s01[:, 0, :], s01[:, 1, :], s23[:, 0, :], s23[:, 1, :]]
-                sqs = []
-                for u in range(U):
-                    sq = sq_pool.tile([P, NB], F32)
-                    nc.scalar.activation(
-                        out=sq[:], in_=t[:, u, :], func=ACT.Square, bias=nb[:, u, j : j + 1], scale=ksq[:, u, j : j + 1]
-                    )
-                    sqs.append(sq)
-                if 2 <= j <= G + 1:
-                    nc.vector.memset(zero[:], 0.0)
+                s_cur = s_pool.tile([P, U, NB], F32)
                 for u in range(U):
                     nc.vector.scalar_tensor_tensor(
-                        out=s_cur[u], in0=tps[u][:], scalar=g[:, u, j : j + 1], in1=sqs[u][:],
+                        out=s_cur[:, u, :], in0=tps[u][:], scalar=g[:, u, j : j + 1], in1=sqs[u][:],
                         op0=ALU.subtract, op1=ALU.mult,
                     )
                 if j == NK - 1 and c + 1 < NCH:
                     tps_next = [turn_x(xs_next, u) for u in range(U)]
-                if 2 <= j <= G + 1:
-                    k = j - 2
-                    nc.gpsimd.tensor_scalar(
-                        out=gate_out[:], in0=zero[:], scalar1=1.0, scalar2=0.0, op0=ALU.mult, op1=ALU.add
-                    )
-                    nc.gpsimd.tensor_tensor(out=lefts[k][:, 0, :], in0=s_older[0], in1=held[k][0][:], op=ALU.subtract)
-                    nc.gpsimd.tensor_tensor(
-                        out=lefts[k][:, 1, 0:GPX1], in0=s_older[1][:, 0:GPX1], in1=held[k][1][:, 0:GPX1], op=ALU.subtract
-                    )
-                if j == 4:
-                    acc0 = acc_psum.tile([P, HALF], F32)
-                    acc1 = acc_psum.tile([P, HALF], F32)
-                    acc = [acc0, acc1]
                 if j >= 4:
                     k = j - 4
                     right = right_pool.tile([P, U, NB], BF16)
-                    inner = []
                     for u in range(U):
-                        right_in = in_pool.tile([P, NB], F32, bufs=4)
-                        nc.scalar.activation(
-                            out=right_in[:], in_=s_prev[u], func=ACT.Relu, scale=e3[:, u, k : k + 1]
-                        )
-                        inner.append(right_in)
-                    if j in Y_STEPS:
-                        a_gp = in_pool.tile([P, NB], F32, bufs=1)
-                        nc.gpsimd.tensor_scalar(
-                            out=a_gp[:, 0:GPY], in0=s_cur[0][:, 0:GPY], scalar1=e4[:, 0, k : k + 1], scalar2=0.0,
-                            op0=ALU.mult, op1=ALU.add,
-                        )
-                        nc.gpsimd.tensor_tensor(
-                            out=right[:, 0, 0:GPY], in0=a_gp[:, 0:GPY], in1=inner[0][:, 0:GPY], op=ALU.subtract
-                        )
-                    for u in range(U):
-                        lo = GPY if (u == 0 and j in Y_STEPS) else 0
                         nc.vector.scalar_tensor_tensor(
-                            out=right[:, u, lo:NB], in0=s_cur[u][:, lo:NB], scalar=e4[:, u, k : k + 1], in1=inner[u][:, lo:NB],
+                            out=right[:, u, :], in0=s_cur[:, u, :], scalar=e4[:, u, k : k + 1], in1=right_in[u][:],
                             op0=ALU.mult, op1=ALU.subtract,
                         )
-                if 1 <= j <= G:
-                    k = j - 1
-                    left = left_pool.tile([P, U, NB], BF16)
-                    lefts[k] = left
-                    left_held0 = in_pool.tile([P, NB], F32, bufs=2)
-                    left_held1 = in_pool.tile([P, NB], F32, bufs=2)
-                    inner = [left_held0, left_held1]
-                    held[k] = inner
-                    for u in range(2, U):
-                        left_in = in_pool.tile([P, NB], F32, bufs=2)
-                        inner.append(left_in)
-                    for u in (1, 2, 3, 0):
-                        nc.scalar.activation(
-                            out=inner[u][:], in_=s_cur[u], func=ACT.Relu, scale=c1[:, u, k : k + 1]
-                        )
-                    for u in range(1, U):
-                        lo = GPX1 if u == 1 else 0
-                        nc.vector.tensor_tensor(
-                            out=left[:, u, lo:NB], in0=s_prev[u][:, lo:NB], in1=inner[u][:, lo:NB], op=ALU.subtract
-                        )
-                if j == 4:
-                    base_grouped = base_pool.tile([P, NB, U], BF16, align_bytes=64)
-                if 4 <= j <= 7:
-                    lo = (j - 4) * (NB // 4)
-                    nc.scalar.activation(
-                        out=by_runs_dst(base_grouped, lo, lo + NB // 4), in_=by_runs_src(t, lo, lo + NB // 4), func=ACT.Silu
-                    )
-                if j >= 4:
-                    k = j - 4
-                    nc.vector.tensor_tensor(out=right[:], in0=lefts[k][:], in1=right[:], op=ALU.max)
-                    made = (right, k, acc, c)
-                s_older = s_prev
-                s_prev = s_cur
+            if left_job is not None:
+                nc.vector.tensor_tensor(
+                    out=flat(left, GX, U * NB), in0=flat(s_first, GX, U * NB), in1=flat(left_in, GX, U * NB), op=ALU.subtract
+                )
+            if live and j >= 4:
+                nc.vector.tensor_tensor(out=right[:], in0=lefts.pop(k)[:], in1=right[:], op=ALU.max)
+                made = (right, k, acc, c)
             if step == 0:
                 prepare_weights()
 
@@ -341,11 +301,9 @@ def tile_kan_layer_t_kernel(tc, x, grid, coef, scale_base, scale_sp, mask, out):
             to_quantise = []
             for grouped, plane, acc_of, c_of in quantised:
                 quantise_and_multiply(grouped, plane, acc_of)
-            if live and j == 7:
-                to_quantise.append((base_grouped, G, acc, c))
             if to_regroup is not None:
                 plane_tile, plane, acc_of, c_of = to_regroup
-                to_quantise.append((regroup(plane_tile, SPLIT[j] if live else 352), plane, acc_of, c_of))
+                to_quantise.append((regroup(plane_tile, BUSY if live and 5 <= j <= G else IDLE if live else HALF), plane, acc_of, c_of))
             to_regroup = made
             if to_store is not None:
                 store(to_store[0], to_store[1])
@@ -356,7 +314,45 @@ def tile_kan_layer_t_kernel(tc, x, grid, coef, scale_base, scale_sp, mask, out):
             for grouped, plane, acc_of, c_of in quantised:
                 if plane == G - 1:
                     to_empty = (acc_of, c_of)
-            if live and c + 1 < NCH and j == NK - 1:
-                t_next = t_pool.tile([P, U, NB], BF16, tag="t")
-                for u in range(U):
-                    nc.scalar.copy(out=t_next[:, u, :], in_=tps_next[u][:])
+
+            if live:
+                if j == G + 2:
+                    base_grouped = base_pool.tile([P, NB, U], BF16, align_bytes=64)
+                    nc.scalar.activation(out=by_runs_dst(base_grouped, 0, NB), in_=by_runs_src(t, 0, NB), func=ACT.Silu)
+                    to_quantise.append((base_grouped, G, acc, c))
+                if j == NK - 1 and c + 1 < NCH:
+                    t_next = t_pool.tile([P, U, NB], BF16, tag="t")
+                    for u in range(U):
+                        nc.scalar.copy(out=t_next[:, u, :], in_=tps_next[u][:])
+                    sqs = squares(t_next, 0)
+                elif j < NK - 1:
+                    sqs = squares(t, j + 1)
+                if 1 <= j <= G:
+                    k = j - 1
+                    left_in = in_pool.tile([P, U, NB], F32)
+                    on_vector = LV if j <= LJ else 0
+                    for u in range(U - on_vector):
+                        nc.scalar.activation(
+                            out=left_in[:, u, :], in_=s_cur[:, u, :], func=ACT.Relu, scale=c1[:, u, k : k + 1]
+                        )
+                    for u in range(U - on_vector, U):
+                        nc.vector.tensor_scalar(
+                            out=left_in[:, u, :], in0=s_cur[:, u, :], scalar1=c1[:, u, k : k + 1], scalar2=0.0,
+                            op0=ALU.mult, op1=ALU.max,
+                        )
+                    left = left_pool.tile([P, U, NB], BF16)
+                    lefts[k] = left
+                    to_left = (s_prev, left_in, left)
+                if 3 <= j <= G + 2:
+                    k = j - 3
+                    right_in = []
+                    for u in range(U):
+                        right_in_u = in_pool.tile([P, NB], F32, bufs=4)
+                        nc.scalar.activation(
+                            out=right_in_u[:], in_=s_cur[:, u, :], func=ACT.Relu, scale=e3[:, u, k : k + 1]
+                        )
+                        right_in.append(right_in_u)
+                s_prev = s_cur
+                if j == NK - 1 and c + 1 < NCH:
+                    t = t_next
+                    tps = tps_next

@@ -19,11 +19,11 @@ NT = NB // P
 NCH = B // NB
 NPL = G + 1
 HALF = 512
-GX = 2048
+GX = 1792
 LV = 2
 LJ = 3
 RUN = 4
-BUSY, IDLE = 512, 768
+BUSY, IDLE = 512, 640
 
 FLOPS = 2 * B * I * O * NPL
 
@@ -135,15 +135,14 @@ def tile_kan_layer_t_kernel(tc, x, grid, coef, scale_base, scale_sp, mask, out):
         nc.vector.tensor_mul(out=e3[:], in0=e3[:], in1=k2[:, :, 3 : G + 3])
         nc.vector.tensor_mul(out=e4[:], in0=e4[:], in1=k2[:, :, 4 : G + 4])
 
-        zero = const.tile([P, 1], F32)
-        gate_out = const.tile([P, 1], F32)
         w_codes = const.tile([P, NPL * O], U32, align_bytes=64)
         w_scales = const.tile([P, NPL * O], U8, align_bytes=64)
 
-        def prepare_weights():
+        def multiply_weights():
             msp = wprep.tile([P, U, O], F32)
             nc.gpsimd.tensor_mul(out=msp[:], in0=mask_sb[:], in1=sp_sb[:])
             coef_v = coef_sb[:].rearrange("p u (o k) -> p k o u", k=G)
+            products = []
             for first, count in ((0, 8), (8, 4)):
                 w_grouped = grp_pool.tile([P, NB, U], BF16, tag="grp", align_bytes=64)
                 w_flat = w_grouped[:].rearrange("p b u -> p (b u)")
@@ -161,6 +160,11 @@ def tile_kan_layer_t_kernel(tc, x, grid, coef, scale_base, scale_sp, mask, out):
                             in1=base_sb[:].rearrange("p u o -> p o u"),
                             op=ALU.mult,
                         )
+                products.append((first, count, w_flat))
+            return products
+
+        def quantise_weights(products):
+            for first, count, w_flat in products:
                 nc.vector.quantize_mx(
                     out=w_codes[:, first * O : (first + count) * O].bitcast(FP8X4),
                     scales=w_scales[:, first * O : (first + count) * O],
@@ -263,10 +267,6 @@ def tile_kan_layer_t_kernel(tc, x, grid, coef, scale_base, scale_sp, mask, out):
 
             if left_job is not None:
                 s_first, left_in, left = left_job
-                nc.vector.memset(zero[:], 0.0)
-                nc.gpsimd.tensor_scalar(
-                    out=gate_out[:], in0=zero[:], scalar1=1.0, scalar2=0.0, op0=ALU.mult, op1=ALU.add
-                )
                 nc.gpsimd.tensor_tensor(
                     out=flat(left, 0, GX), in0=flat(s_first, 0, GX), in1=flat(left_in, 0, GX), op=ALU.subtract
                 )
@@ -291,16 +291,18 @@ def tile_kan_layer_t_kernel(tc, x, grid, coef, scale_base, scale_sp, mask, out):
                 nc.vector.tensor_tensor(
                     out=flat(left, GX, U * NB), in0=flat(s_first, GX, U * NB), in1=flat(left_in, GX, U * NB), op=ALU.subtract
                 )
-            if live and j >= 4:
-                nc.vector.tensor_tensor(out=right[:], in0=lefts.pop(k)[:], in1=right[:], op=ALU.max)
-                made = (right, k, acc, c)
             if step == 0:
-                prepare_weights()
+                products = multiply_weights()
+            if step == 3:
+                quantise_weights(products)
 
             quantised = to_quantise
             to_quantise = []
             for grouped, plane, acc_of, c_of in quantised:
                 quantise_and_multiply(grouped, plane, acc_of)
+            if live and j >= 4:
+                nc.vector.tensor_tensor(out=right[:], in0=lefts.pop(k)[:], in1=right[:], op=ALU.max)
+                made = (right, k, acc, c)
             if to_regroup is not None:
                 plane_tile, plane, acc_of, c_of = to_regroup
                 to_quantise.append((regroup(plane_tile, BUSY if live and 5 <= j <= G else IDLE if live else HALF), plane, acc_of, c_of))

@@ -20,10 +20,10 @@ NCH = B // NB
 NPL = G + 1
 HALF = 512
 GX = 1792
-LV = 2
-LJ = 3
 RUN = 4
-BUSY, IDLE = 512, 640
+BUSY, IDLE = 512, 256
+NEG = 7
+LATE = 8
 
 FLOPS = 2 * B * I * O * NPL
 
@@ -40,7 +40,7 @@ def tile_kan_layer_t_kernel(tc, x, grid, coef, scale_base, scale_sp, mask, out):
         sq_pool = ctx.enter_context(tc.tile_pool(name="sq", bufs=4))
         in_pool = ctx.enter_context(tc.tile_pool(name="inner", bufs=1))
         left_pool = ctx.enter_context(tc.tile_pool(name="left", bufs=3))
-        right_pool = ctx.enter_context(tc.tile_pool(name="right", bufs=2))
+        right_pool = ctx.enter_context(tc.tile_pool(name="right", bufs=3))
         grp_pool = ctx.enter_context(tc.tile_pool(name="grp", bufs=2))
         base_pool = ctx.enter_context(tc.tile_pool(name="base", bufs=1))
         q_pool = ctx.enter_context(tc.tile_pool(name="q", bufs=2))
@@ -75,7 +75,7 @@ def tile_kan_layer_t_kernel(tc, x, grid, coef, scale_base, scale_sp, mask, out):
         nc.sync.dma_start(out=sp_sb[:], in_=scale_sp.rearrange("(u p) o -> p u o", p=P))
         base_sb = wprep.tile([P, U, O], BF16)
         nc.sync.dma_start(out=base_sb[:], in_=scale_base.rearrange("(u p) o -> p u o", p=P))
-        coef_sb = wprep.tile([P, U, O * G], BF16)
+        coef_sb = s_pool.tile([P, U, O * G], BF16, tag="s")
         nc.sync.dma_start(out=coef_sb[:], in_=coef.rearrange("(u p) o k -> p u (o k)", p=P))
 
         g = const.tile([P, U, NK], F32)
@@ -101,40 +101,43 @@ def tile_kan_layer_t_kernel(tc, x, grid, coef, scale_base, scale_sp, mask, out):
             return acc
 
         c0 = product("c0", [d1[:, :, 0:G], d2[:, :, 0:G], d3[:, :, 0:G]])
-        nc.vector.reciprocal(out=c0[:], in_=c0[:])
-        kap = const.tile([P, U, G], F32)
-        nc.scalar.activation(out=kap[:], in_=c0[:], func=ACT.Sqrt)
+        e4 = product("e4", [d3[:, :, 1 : G + 1], d2[:, :, 2 : G + 2], d1[:, :, 3 : G + 3]])
+        k2 = const.tile([P, U, NK], F32)
+        nc.vector.tensor_copy(out=k2[:, :, 0:G], in_=c0[:])
+        nc.vector.tensor_copy(out=k2[:, :, G:NK], in_=e4[:, :, NEG:G])
         ksq = const.tile([P, U, NK], F32)
-        nc.vector.memset(ksq[:], 1.0)
+        nc.vector.reciprocal(out=ksq[:], in_=k2[:])
+        kap = const.tile([P, U, NK], F32)
+        nc.scalar.activation(out=kap[:], in_=ksq[:], func=ACT.Sqrt)
         t_first = t_pool.tile([P, U, NB], BF16, tag="t")
         tps_next = []
         for u in range(U):
             tps_next.append(turn_x(xs0, u))
             nc.scalar.copy(out=t_first[:, u, :], in_=tps_next[u][:])
+        rk = const.tile([P, U, NK], F32)
+        nc.vector.reciprocal(out=rk[:], in_=kap[:])
+        nc.vector.tensor_mul(out=ksq[:], in0=rk[:], in1=ksq[:])
+        nc.vector.tensor_add(out=ksq[:], in0=ksq[:], in1=kap[:])
+        nc.vector.tensor_scalar_mul(out=ksq[:], in0=ksq[:], scalar1=0.5)
+        nb = const.tile([P, U, NK], F32)
+        nc.vector.tensor_mul(out=nb[:], in0=ksq[:], in1=neg_g[:])
+        nc.vector.tensor_mul(out=k2[:], in0=ksq[:], in1=ksq[:])
+        nc.vector.reciprocal(out=k2[:], in_=k2[:])
         c1 = product("c1", [d1[:, :, 0:G], d1[:, :, 1 : G + 1], d2[:, :, 1 : G + 1], d3[:, :, 1 : G + 1]])
         nc.vector.reciprocal(out=c1[:], in_=c1[:])
         nc.vector.tensor_mul(out=c1[:], in0=c1[:], in1=d4[:])
-        e4 = product("e4", [d3[:, :, 1 : G + 1], d2[:, :, 2 : G + 2], d1[:, :, 3 : G + 3]])
+        nc.vector.tensor_mul(out=c1[:], in0=c1[:], in1=k2[:, :, 1 : G + 1])
         nc.vector.reciprocal(out=e4[:], in_=e4[:])
         nc.vector.tensor_scalar_mul(out=e4[:], in0=e4[:], scalar1=-1.0)
+        nc.vector.tensor_mul(out=e4[:], in0=e4[:], in1=k2[:, :, 4 : G + 4])
         e3 = product("e3", [d3[:, :, 0:G], d2[:, :, 1 : G + 1], d1[:, :, 2 : G + 2], d1[:, :, 3 : G + 3]])
         nc.vector.reciprocal(out=e3[:], in_=e3[:])
         nc.vector.tensor_mul(out=e3[:], in0=e3[:], in1=d4[:])
         nc.vector.tensor_scalar_mul(out=e3[:], in0=e3[:], scalar1=-1.0)
-        rk = const.tile([P, U, G], F32)
-        nc.vector.reciprocal(out=rk[:], in_=kap[:])
-        nc.vector.tensor_mul(out=rk[:], in0=rk[:], in1=c0[:])
-        nc.vector.tensor_add(out=rk[:], in0=rk[:], in1=kap[:])
-        nc.vector.tensor_scalar_mul(out=ksq[:, :, 0:G], in0=rk[:], scalar1=0.5)
-        nb = const.tile([P, U, NK], F32)
-        nc.vector.tensor_mul(out=nb[:], in0=ksq[:], in1=neg_g[:])
-        k2 = const.tile([P, U, NK], F32)
-        nc.vector.tensor_mul(out=k2[:], in0=ksq[:], in1=ksq[:])
-        nc.vector.reciprocal(out=k2[:], in_=k2[:])
-        nc.vector.tensor_mul(out=c1[:], in0=c1[:], in1=k2[:, :, 1 : G + 1])
         nc.vector.tensor_mul(out=e3[:], in0=e3[:], in1=k2[:, :, 3 : G + 3])
-        nc.vector.tensor_mul(out=e4[:], in0=e4[:], in1=k2[:, :, 4 : G + 4])
 
+        zero = const.tile([P, 1], F32)
+        gate_out = const.tile([P, 1], F32)
         w_codes = const.tile([P, NPL * O], U32, align_bytes=64)
         w_scales = const.tile([P, NPL * O], U8, align_bytes=64)
 
@@ -196,15 +199,16 @@ def tile_kan_layer_t_kernel(tc, x, grid, coef, scale_base, scale_sp, mask, out):
                     stop=(plane == G - 1),
                 )
 
-        def regroup(plane_tile, sc):
+        def regroup(plane_tile, sign, sc):
             grouped = grp_pool.tile([P, NB, U], BF16, tag="grp", align_bytes=64)
             if sc > 0:
                 nc.scalar.activation(
-                    out=by_runs_dst(grouped, 0, sc), in_=by_runs_src(plane_tile, 0, sc), func=ACT.Relu
+                    out=by_runs_dst(grouped, 0, sc), in_=by_runs_src(plane_tile, 0, sc), func=ACT.Relu, scale=sign
                 )
             if sc < NB:
-                nc.vector.tensor_scalar_max(
-                    out=by_runs_dst(grouped, sc, NB), in0=by_runs_src(plane_tile, sc, NB), scalar1=0.0
+                nc.vector.tensor_scalar(
+                    out=by_runs_dst(grouped, sc, NB), in0=by_runs_src(plane_tile, sc, NB), scalar1=sign, scalar2=0.0,
+                    op0=ALU.mult, op1=ALU.max,
                 )
             return grouped
 
@@ -240,7 +244,14 @@ def tile_kan_layer_t_kernel(tc, x, grid, coef, scale_base, scale_sp, mask, out):
         def flat(tile, lo, hi):
             return tile[:].rearrange("p u b -> p (u b)")[:, lo:hi]
 
+        def combine(engine, lo, hi, job):
+            half, in0, in1, op = job
+            engine.tensor_tensor(out=flat(half, lo, hi), in0=flat(in0, lo, hi), in1=flat(in1, lo, hi), op=op)
+
+        ALL = U * NB
         to_left = None
+        on_gpsimd = {}
+        merges = {}
         to_regroup = None
         to_quantise = []
         to_empty = None
@@ -251,27 +262,31 @@ def tile_kan_layer_t_kernel(tc, x, grid, coef, scale_base, scale_sp, mask, out):
         s_prev = None
         right_in = None
         lefts = {}
+        accs = {}
 
-        for step in range(NCH * NK + 4):
+        for step in range(NCH * NK + 5):
             c, j = divmod(step, NK)
             live = c < NCH
-            made = None
             left_job = to_left
             to_left = None
-            if live and j == 4:
+            if live and j == 5:
                 acc0 = acc_psum.tile([P, HALF], F32)
                 acc1 = acc_psum.tile([P, HALF], F32)
-                acc = [acc0, acc1]
+                accs[c] = [acc0, acc1]
             if live and j == 0 and c + 1 < NCH:
                 xs_next = load_x(c + 1)
 
             if left_job is not None:
-                s_first, left_in, left = left_job
-                nc.gpsimd.tensor_tensor(
-                    out=flat(left, 0, GX), in0=flat(s_first, 0, GX), in1=flat(left_in, 0, GX), op=ALU.subtract
+                combine(nc.gpsimd, 0, GX, left_job)
+            if step in on_gpsimd:
+                nc.gpsimd.tensor_scalar(
+                    out=gate_out[:], in0=zero[:], scalar1=1.0, scalar2=0.0, op0=ALU.mult, op1=ALU.add
                 )
+                lo, hi, job = on_gpsimd[step]
+                combine(nc.gpsimd, lo, hi, job)
+
             if live:
-                s_cur = s_pool.tile([P, U, NB], F32)
+                s_cur = s_pool.tile([P, U, NB], F32, tag="s")
                 for u in range(U):
                     nc.vector.scalar_tensor_tensor(
                         out=s_cur[:, u, :], in0=tps[u][:], scalar=g[:, u, j : j + 1], in1=sqs[u][:],
@@ -282,46 +297,67 @@ def tile_kan_layer_t_kernel(tc, x, grid, coef, scale_base, scale_sp, mask, out):
                 if j >= 4:
                     k = j - 4
                     right = right_pool.tile([P, U, NB], BF16)
-                    for u in range(U):
-                        nc.vector.scalar_tensor_tensor(
-                            out=right[:, u, :], in0=s_cur[:, u, :], scalar=e4[:, u, k : k + 1], in1=right_in[u][:],
-                            op0=ALU.mult, op1=ALU.subtract,
-                        )
+                    wait = 0
+                    if k < NEG:
+                        for u in range(U):
+                            nc.vector.scalar_tensor_tensor(
+                                out=right[:, u, :], in0=s_cur[:, u, :], scalar=e4[:, u, k : k + 1], in1=right_in[:, u, :],
+                                op0=ALU.mult, op1=ALU.subtract,
+                            )
+                    else:
+                        job = (right, s_cur, right_in, ALU.add)
+                        lo = 0
+                        if k >= LATE:
+                            wait = 1
+                            if step + 1 < NCH * NK:
+                                lo = GX
+                                on_gpsimd[step + 1] = (0, GX, job)
+                                if k == G - 1:
+                                    lo = ALL
+                                    wait = 2
+                                    on_gpsimd[step + 2] = (GX, ALL, job)
+                        if lo < ALL:
+                            combine(nc.vector, lo, ALL, job)
+                    merges[step + wait] = (right, k, c)
             if left_job is not None:
-                nc.vector.tensor_tensor(
-                    out=flat(left, GX, U * NB), in0=flat(s_first, GX, U * NB), in1=flat(left_in, GX, U * NB), op=ALU.subtract
-                )
+                combine(nc.vector, GX, ALL, left_job)
             if step == 0:
                 products = multiply_weights()
             if step == 3:
                 quantise_weights(products)
-
             quantised = to_quantise
             to_quantise = []
-            for grouped, plane, acc_of, c_of in quantised:
-                quantise_and_multiply(grouped, plane, acc_of)
-            if live and j >= 4:
-                nc.vector.tensor_tensor(out=right[:], in0=lefts.pop(k)[:], in1=right[:], op=ALU.max)
-                made = (right, k, acc, c)
+            for grouped, plane, c_of in quantised:
+                quantise_and_multiply(grouped, plane, accs[c_of])
+            made = None
+            if step in merges:
+                right_of, plane, c_of = merges[step]
+                nc.vector.tensor_tensor(
+                    out=right_of[:], in0=lefts[c_of, plane][:], in1=right_of[:], op=ALU.max if plane < NEG else ALU.min
+                )
+                made = (right_of, plane, c_of)
+            if step + 1 in on_gpsimd:
+                nc.vector.memset(zero[:], 0.0)
             if to_regroup is not None:
-                plane_tile, plane, acc_of, c_of = to_regroup
-                to_quantise.append((regroup(plane_tile, BUSY if live and 5 <= j <= G else IDLE if live else HALF), plane, acc_of, c_of))
+                plane_tile, plane, c_of = to_regroup
+                share = BUSY if live and 5 <= j <= G else IDLE if live else HALF
+                to_quantise.append((regroup(plane_tile, 1.0 if plane < NEG else -1.0, share), plane, c_of))
             to_regroup = made
             if to_store is not None:
                 store(to_store[0], to_store[1])
                 to_store = None
             if to_empty is not None:
-                to_store = (empty_sums(to_empty[0]), to_empty[1])
+                to_store = (empty_sums(accs[to_empty]), to_empty)
                 to_empty = None
-            for grouped, plane, acc_of, c_of in quantised:
+            for grouped, plane, c_of in quantised:
                 if plane == G - 1:
-                    to_empty = (acc_of, c_of)
+                    to_empty = c_of
 
             if live:
                 if j == G + 2:
                     base_grouped = base_pool.tile([P, NB, U], BF16, align_bytes=64)
                     nc.scalar.activation(out=by_runs_dst(base_grouped, 0, NB), in_=by_runs_src(t, 0, NB), func=ACT.Silu)
-                    to_quantise.append((base_grouped, G, acc, c))
+                    to_quantise.append((base_grouped, G, c))
                 if j == NK - 1 and c + 1 < NCH:
                     t_next = t_pool.tile([P, U, NB], BF16, tag="t")
                     for u in range(U):
@@ -332,28 +368,20 @@ def tile_kan_layer_t_kernel(tc, x, grid, coef, scale_base, scale_sp, mask, out):
                 if 1 <= j <= G:
                     k = j - 1
                     left_in = in_pool.tile([P, U, NB], F32)
-                    on_vector = LV if j <= LJ else 0
-                    for u in range(U - on_vector):
+                    for u in range(U):
                         nc.scalar.activation(
                             out=left_in[:, u, :], in_=s_cur[:, u, :], func=ACT.Relu, scale=c1[:, u, k : k + 1]
                         )
-                    for u in range(U - on_vector, U):
-                        nc.vector.tensor_scalar(
-                            out=left_in[:, u, :], in0=s_cur[:, u, :], scalar1=c1[:, u, k : k + 1], scalar2=0.0,
-                            op0=ALU.mult, op1=ALU.max,
-                        )
                     left = left_pool.tile([P, U, NB], BF16)
-                    lefts[k] = left
-                    to_left = (s_prev, left_in, left)
+                    lefts[c, k] = left
+                    to_left = (left, s_prev, left_in, ALU.subtract) if k < NEG else (left, left_in, s_prev, ALU.subtract)
                 if 3 <= j <= G + 2:
                     k = j - 3
-                    right_in = []
+                    right_in = in_pool.tile([P, U, NB], F32, bufs=2)
                     for u in range(U):
-                        right_in_u = in_pool.tile([P, NB], F32, bufs=4)
                         nc.scalar.activation(
-                            out=right_in_u[:], in_=s_cur[:, u, :], func=ACT.Relu, scale=e3[:, u, k : k + 1]
+                            out=right_in[:, u, :], in_=s_cur[:, u, :], func=ACT.Relu, scale=e3[:, u, k : k + 1]
                         )
-                        right_in.append(right_in_u)
                 s_prev = s_cur
                 if j == NK - 1 and c + 1 < NCH:
                     t = t_next

@@ -21,7 +21,7 @@ NPL = G + 1
 HALF = 512
 GX = 1792
 RUN = 4
-BUSY, IDLE = 512, 256
+BUSY = 512
 NEG = 7
 LATE = 8
 
@@ -199,16 +199,15 @@ def tile_kan_layer_t_kernel(tc, x, grid, coef, scale_base, scale_sp, mask, out):
                     stop=(plane == G - 1),
                 )
 
-        def regroup(plane_tile, sign, sc):
+        def regroup(plane_tile, sc):
             grouped = grp_pool.tile([P, NB, U], BF16, tag="grp", align_bytes=64)
             if sc > 0:
                 nc.scalar.activation(
-                    out=by_runs_dst(grouped, 0, sc), in_=by_runs_src(plane_tile, 0, sc), func=ACT.Relu, scale=sign
+                    out=by_runs_dst(grouped, 0, sc), in_=by_runs_src(plane_tile, 0, sc), func=ACT.Relu
                 )
             if sc < NB:
-                nc.vector.tensor_scalar(
-                    out=by_runs_dst(grouped, sc, NB), in0=by_runs_src(plane_tile, sc, NB), scalar1=sign, scalar2=0.0,
-                    op0=ALU.mult, op1=ALU.max,
+                nc.vector.tensor_scalar_max(
+                    out=by_runs_dst(grouped, sc, NB), in0=by_runs_src(plane_tile, sc, NB), scalar1=0.0
                 )
             return grouped
 
@@ -245,8 +244,14 @@ def tile_kan_layer_t_kernel(tc, x, grid, coef, scale_base, scale_sp, mask, out):
             return tile[:].rearrange("p u b -> p (u b)")[:, lo:hi]
 
         def combine(engine, lo, hi, job):
-            half, in0, in1, op = job
-            engine.tensor_tensor(out=flat(half, lo, hi), in0=flat(in0, lo, hi), in1=flat(in1, lo, hi), op=op)
+            half, in0, in1, op, woven = job
+            if woven:
+                lo, hi = lo // U, hi // U
+                engine.tensor_tensor(
+                    out=by_runs_dst(half, lo, hi), in0=by_runs_src(in0, lo, hi), in1=by_runs_src(in1, lo, hi), op=op
+                )
+            else:
+                engine.tensor_tensor(out=flat(half, lo, hi), in0=flat(in0, lo, hi), in1=flat(in1, lo, hi), op=op)
 
         ALL = U * NB
         to_left = None
@@ -296,16 +301,17 @@ def tile_kan_layer_t_kernel(tc, x, grid, coef, scale_base, scale_sp, mask, out):
                     tps_next = [turn_x(xs_next, u) for u in range(U)]
                 if j >= 4:
                     k = j - 4
-                    right = right_pool.tile([P, U, NB], BF16)
                     wait = 0
                     if k < NEG:
+                        right = right_pool.tile([P, U, NB], BF16, tag="right", align_bytes=64)
                         for u in range(U):
                             nc.vector.scalar_tensor_tensor(
                                 out=right[:, u, :], in0=s_cur[:, u, :], scalar=e4[:, u, k : k + 1], in1=right_in[:, u, :],
                                 op0=ALU.mult, op1=ALU.subtract,
                             )
                     else:
-                        job = (right, s_cur, right_in, ALU.add)
+                        right = right_pool.tile([P, NB, U], BF16, tag="right", align_bytes=64)
+                        job = (right, s_cur, right_in, ALU.add, True)
                         lo = 0
                         if k >= LATE:
                             wait = 1
@@ -340,8 +346,15 @@ def tile_kan_layer_t_kernel(tc, x, grid, coef, scale_base, scale_sp, mask, out):
                 nc.vector.memset(zero[:], 0.0)
             if to_regroup is not None:
                 plane_tile, plane, c_of = to_regroup
-                share = BUSY if live and 5 <= j <= G else IDLE if live else HALF
-                to_quantise.append((regroup(plane_tile, 1.0 if plane < NEG else -1.0, share), plane, c_of))
+                share = BUSY
+                if plane < NEG:
+                    to_quantise.append((regroup(plane_tile, share), plane, c_of))
+                else:
+                    flipped = grp_pool.tile([P, NB, U], BF16, tag="grp", align_bytes=64)
+                    nc.vector.tensor_scalar(
+                        out=flipped[:], in0=plane_tile[:], scalar1=-1.0, scalar2=0.0, op0=ALU.mult, op1=ALU.max
+                    )
+                    to_quantise.append((flipped, plane, c_of))
             to_regroup = made
             if to_store is not None:
                 store(to_store[0], to_store[1])
@@ -372,9 +385,13 @@ def tile_kan_layer_t_kernel(tc, x, grid, coef, scale_base, scale_sp, mask, out):
                         nc.scalar.activation(
                             out=left_in[:, u, :], in_=s_cur[:, u, :], func=ACT.Relu, scale=c1[:, u, k : k + 1]
                         )
-                    left = left_pool.tile([P, U, NB], BF16)
+                    if k < NEG:
+                        left = left_pool.tile([P, U, NB], BF16, tag="left")
+                        to_left = (left, s_prev, left_in, ALU.subtract, False)
+                    else:
+                        left = left_pool.tile([P, NB, U], BF16, tag="left")
+                        to_left = (left, left_in, s_prev, ALU.subtract, True)
                     lefts[c, k] = left
-                    to_left = (left, s_prev, left_in, ALU.subtract) if k < NEG else (left, left_in, s_prev, ALU.subtract)
                 if 3 <= j <= G + 2:
                     k = j - 3
                     right_in = in_pool.tile([P, U, NB], F32, bufs=2)

@@ -21,7 +21,7 @@ NPL = G + 1
 HALF = 512
 GX = 1792
 RUN = 4
-BUSY = 512
+BUSY = 448
 NEG = 7
 LATE = 8
 
@@ -201,15 +201,16 @@ def tile_kan_layer_t_kernel(tc, x, grid, coef, scale_base, scale_sp, mask, out):
 
         def regroup(plane_tile, sc):
             grouped = grp_pool.tile([P, NB, U], BF16, tag="grp", align_bytes=64)
-            if sc > 0:
-                nc.scalar.activation(
-                    out=by_runs_dst(grouped, 0, sc), in_=by_runs_src(plane_tile, 0, sc), func=ACT.Relu
-                )
             if sc < NB:
                 nc.vector.tensor_scalar_max(
                     out=by_runs_dst(grouped, sc, NB), in0=by_runs_src(plane_tile, sc, NB), scalar1=0.0
                 )
             return grouped
+
+        def regroup_on_scalar(plane_tile, grouped, sc):
+            nc.scalar.activation(
+                out=by_runs_dst(grouped, 0, sc), in_=by_runs_src(plane_tile, 0, sc), func=ACT.Relu
+            )
 
         def empty_sums(acc):
             out_t = o_pool.tile([P, NB], F32)
@@ -299,6 +300,8 @@ def tile_kan_layer_t_kernel(tc, x, grid, coef, scale_base, scale_sp, mask, out):
                     )
                 if j == NK - 1 and c + 1 < NCH:
                     tps_next = [turn_x(xs_next, u) for u in range(U)]
+                if left_job is not None:
+                    combine(nc.vector, GX, ALL, left_job)
                 if j >= 4:
                     k = j - 4
                     wait = 0
@@ -325,8 +328,6 @@ def tile_kan_layer_t_kernel(tc, x, grid, coef, scale_base, scale_sp, mask, out):
                         if lo < ALL:
                             combine(nc.vector, lo, ALL, job)
                     merges[step + wait] = (right, k, c)
-            if left_job is not None:
-                combine(nc.vector, GX, ALL, left_job)
             if step == 0:
                 products = multiply_weights()
             if step == 3:
@@ -344,11 +345,14 @@ def tile_kan_layer_t_kernel(tc, x, grid, coef, scale_base, scale_sp, mask, out):
                 made = (right_of, plane, c_of)
             if step + 1 in on_gpsimd:
                 nc.vector.memset(zero[:], 0.0)
+            rest = None
             if to_regroup is not None:
                 plane_tile, plane, c_of = to_regroup
                 share = BUSY
                 if plane < NEG:
-                    to_quantise.append((regroup(plane_tile, share), plane, c_of))
+                    grouped = regroup(plane_tile, share)
+                    to_quantise.append((grouped, plane, c_of))
+                    rest = (plane_tile, grouped, share)
                 else:
                     flipped = grp_pool.tile([P, NB, U], BF16, tag="grp", align_bytes=64)
                     nc.vector.tensor_scalar(
@@ -399,6 +403,8 @@ def tile_kan_layer_t_kernel(tc, x, grid, coef, scale_base, scale_sp, mask, out):
                         nc.scalar.activation(
                             out=right_in[:, u, :], in_=s_cur[:, u, :], func=ACT.Relu, scale=e3[:, u, k : k + 1]
                         )
+                if rest is not None:
+                    regroup_on_scalar(*rest)
                 s_prev = s_cur
                 if j == NK - 1 and c + 1 < NCH:
                     t = t_next

@@ -21,7 +21,7 @@ NPL = G + 1
 HALF = 512
 GX = 1792
 RUN = 4
-BUSY = 448
+BUSY = 480
 NEG = 7
 LATE = 8
 
@@ -109,11 +109,7 @@ def tile_kan_layer_t_kernel(tc, x, grid, coef, scale_base, scale_sp, mask, out):
         nc.vector.reciprocal(out=ksq[:], in_=k2[:])
         kap = const.tile([P, U, NK], F32)
         nc.scalar.activation(out=kap[:], in_=ksq[:], func=ACT.Sqrt)
-        t_first = t_pool.tile([P, U, NB], BF16, tag="t")
-        tps_next = []
-        for u in range(U):
-            tps_next.append(turn_x(xs0, u))
-            nc.scalar.copy(out=t_first[:, u, :], in_=tps_next[u][:])
+        tps_next = [turn_x(xs0, u) for u in range(U)]
         rk = const.tile([P, U, NK], F32)
         nc.vector.reciprocal(out=rk[:], in_=kap[:])
         nc.vector.tensor_mul(out=ksq[:], in0=rk[:], in1=ksq[:])
@@ -231,9 +227,11 @@ def tile_kan_layer_t_kernel(tc, x, grid, coef, scale_base, scale_sp, mask, out):
             nc.vector.tensor_copy(out=out_sb[:, 4:8, :], in_=turned[1][:])
             nc.sync.dma_start(out=out[c * NB : (c + 1) * NB, :].rearrange("(p n) o -> p n o", n=NT), in_=out_sb[:])
 
-        def squares(t, j):
+        def squares(t, j, source=None):
             sqs = []
             for u in range(U):
+                if source is not None:
+                    nc.scalar.copy(out=t[:, u, :], in_=source[u][:])
                 sq = sq_pool.tile([P, NB], F32)
                 nc.scalar.activation(
                     out=sq[:], in_=t[:, u, :], func=ACT.Square, bias=nb[:, u, j : j + 1], scale=ksq[:, u, j : j + 1]
@@ -262,9 +260,9 @@ def tile_kan_layer_t_kernel(tc, x, grid, coef, scale_base, scale_sp, mask, out):
         to_quantise = []
         to_empty = None
         to_store = None
-        t = t_first
+        t = t_pool.tile([P, U, NB], BF16)
         tps = tps_next
-        sqs = squares(t, 0)
+        sqs = squares(t, 0, tps)
         s_prev = None
         right_in = None
         lefts = {}
@@ -355,20 +353,14 @@ def tile_kan_layer_t_kernel(tc, x, grid, coef, scale_base, scale_sp, mask, out):
                     rest = (plane_tile, grouped, share)
                 else:
                     flipped = grp_pool.tile([P, NB, U], BF16, tag="grp", align_bytes=64)
-                    nc.vector.tensor_scalar(
-                        out=flipped[:], in0=plane_tile[:], scalar1=-1.0, scalar2=0.0, op0=ALU.mult, op1=ALU.max
-                    )
+                    if live or plane == G - 1:
+                        nc.vector.tensor_scalar(
+                            out=flipped[:], in0=plane_tile[:], scalar1=-1.0, scalar2=0.0, op0=ALU.mult, op1=ALU.max
+                        )
+                    else:
+                        nc.scalar.activation(out=flipped[:], in_=plane_tile[:], func=ACT.Relu, scale=-1.0)
                     to_quantise.append((flipped, plane, c_of))
             to_regroup = made
-            if to_store is not None:
-                store(to_store[0], to_store[1])
-                to_store = None
-            if to_empty is not None:
-                to_store = (empty_sums(accs[to_empty]), to_empty)
-                to_empty = None
-            for grouped, plane, c_of in quantised:
-                if plane == G - 1:
-                    to_empty = c_of
 
             if live:
                 if j == G + 2:
@@ -376,10 +368,9 @@ def tile_kan_layer_t_kernel(tc, x, grid, coef, scale_base, scale_sp, mask, out):
                     nc.scalar.activation(out=by_runs_dst(base_grouped, 0, NB), in_=by_runs_src(t, 0, NB), func=ACT.Silu)
                     to_quantise.append((base_grouped, G, c))
                 if j == NK - 1 and c + 1 < NCH:
-                    t_next = t_pool.tile([P, U, NB], BF16, tag="t")
-                    for u in range(U):
-                        nc.scalar.copy(out=t_next[:, u, :], in_=tps_next[u][:])
-                    sqs = squares(t_next, 0)
+                    t = t_pool.tile([P, U, NB], BF16)
+                    tps = tps_next
+                    sqs = squares(t, 0, tps)
                 elif j < NK - 1:
                     sqs = squares(t, j + 1)
                 if 1 <= j <= G:
@@ -406,6 +397,12 @@ def tile_kan_layer_t_kernel(tc, x, grid, coef, scale_base, scale_sp, mask, out):
                 if rest is not None:
                     regroup_on_scalar(*rest)
                 s_prev = s_cur
-                if j == NK - 1 and c + 1 < NCH:
-                    t = t_next
-                    tps = tps_next
+            if to_store is not None:
+                store(to_store[0], to_store[1])
+                to_store = None
+            if to_empty is not None:
+                to_store = (empty_sums(accs[to_empty]), to_empty)
+                to_empty = None
+            for grouped, plane, c_of in quantised:
+                if plane == G - 1:
+                    to_empty = c_of

from contextlib import ExitStack

import concourse.mybir as mybir
from concourse.masks import make_identity

F32 = mybir.dt.float32
BF16 = mybir.dt.bfloat16
U32 = mybir.dt.uint32
U8 = mybir.dt.uint8
FP8X4 = mybir.dt.float8_e4m3fn_x4
ACT = mybir.ActivationFunctionType
ALU = mybir.AluOpType

B, I, O, G, NK = 4096, 512, 128, 11, 15
P = 128
U = I // P
NB = 1024
NT = NB // P
NCH = B // NB
NPL = G + 1
HALF = 512
GX = 1792
RUN = 4
BUSY = 480
NEG = 7
LATE = 8

FLOPS = 2 * B * I * O * NPL


def tile_kan_layer_t_kernel(tc, x, grid, coef, scale_base, scale_sp, mask, out):
    nc = tc.nc
    with ExitStack() as ctx:
        ctx.enter_context(tc.manual_schedule())
        const = ctx.enter_context(tc.tile_pool(name="const", bufs=1))
        wprep = ctx.enter_context(tc.tile_pool(name="wprep", bufs=1))
        xs_pool = ctx.enter_context(tc.tile_pool(name="xs", bufs=1))
        t_pool = ctx.enter_context(tc.tile_pool(name="t", bufs=1))
        s_pool = ctx.enter_context(tc.tile_pool(name="s", bufs=3))
        sq_pool = ctx.enter_context(tc.tile_pool(name="sq", bufs=4))
        in_pool = ctx.enter_context(tc.tile_pool(name="inner", bufs=1))
        left_pool = ctx.enter_context(tc.tile_pool(name="left", bufs=3))
        right_pool = ctx.enter_context(tc.tile_pool(name="right", bufs=3))
        grp_pool = ctx.enter_context(tc.tile_pool(name="grp", bufs=2))
        base_pool = ctx.enter_context(tc.tile_pool(name="base", bufs=1))
        q_pool = ctx.enter_context(tc.tile_pool(name="q", bufs=2))
        o_pool = ctx.enter_context(tc.tile_pool(name="o", bufs=1))
        tp_psum = ctx.enter_context(tc.psum_pool(name="tp", bufs=1))
        acc_psum = ctx.enter_context(tc.psum_pool(name="acc", bufs=1))
        ot_psum = ctx.enter_context(tc.psum_pool(name="ot", bufs=2))

        ident_bf = const.tile([P, P], BF16)
        make_identity(nc, ident_bf[:])
        ident_f = const.tile([P, P], F32)
        make_identity(nc, ident_f[:])

        g_bf = const.tile([P, U, NK], BF16)
        nc.sync.dma_start(out=g_bf[:], in_=grid.rearrange("(u p) j -> p u j", p=P))

        def load_x(c):
            xs = xs_pool.tile([P, NT, I], BF16)
            nc.sync.dma_start(out=xs[:], in_=x[c * NB : (c + 1) * NB, :].rearrange("(p n) i -> p n i", n=NT))
            return xs

        def turn_x(xs, u):
            tp = tp_psum.tile([P, NB], BF16, name="tp%d" % u)
            for n in range(NT):
                nc.tensor.transpose(tp[:, n * P : (n + 1) * P], xs[:, n, u * P : (u + 1) * P], ident_bf[:])
            return tp

        xs0 = load_x(0)
        mask_sb = wprep.tile([P, U, O], BF16)
        nc.sync.dma_start(out=mask_sb[:], in_=mask.rearrange("(u p) o -> p u o", p=P))
        sp_sb = wprep.tile([P, U, O], BF16)
        nc.sync.dma_start(out=sp_sb[:], in_=scale_sp.rearrange("(u p) o -> p u o", p=P))
        base_sb = wprep.tile([P, U, O], BF16)
        nc.sync.dma_start(out=base_sb[:], in_=scale_base.rearrange("(u p) o -> p u o", p=P))
        coef_sb = s_pool.tile([P, U, O * G], BF16, tag="s")
        nc.sync.dma_start(out=coef_sb[:], in_=coef.rearrange("(u p) o k -> p u (o k)", p=P))

        g = const.tile([P, U, NK], F32)
        nc.vector.tensor_copy(out=g[:], in_=g_bf[:])
        neg_g = const.tile([P, U, NK], F32)
        nc.vector.tensor_scalar_mul(out=neg_g[:], in0=g[:], scalar1=-1.0)


        d1 = const.tile([P, U, NK - 1], F32)
        nc.vector.tensor_sub(out=d1[:], in0=g[:, :, 1:NK], in1=g[:, :, 0 : NK - 1])
        d2 = const.tile([P, U, NK - 2], F32)
        nc.vector.tensor_sub(out=d2[:], in0=g[:, :, 2:NK], in1=g[:, :, 0 : NK - 2])
        d3 = const.tile([P, U, NK - 3], F32)
        nc.vector.tensor_sub(out=d3[:], in0=g[:, :, 3:NK], in1=g[:, :, 0 : NK - 3])
        d4 = const.tile([P, U, NK - 4], F32)
        nc.vector.tensor_sub(out=d4[:], in0=g[:, :, 4:NK], in1=g[:, :, 0 : NK - 4])

        def product(name, factors):
            acc = const.tile([P, U, G], F32, name=name)
            nc.vector.tensor_mul(out=acc[:], in0=factors[0], in1=factors[1])
            for f in factors[2:]:
                nc.vector.tensor_mul(out=acc[:], in0=acc[:], in1=f)
            return acc

        c0 = product("c0", [d1[:, :, 0:G], d2[:, :, 0:G], d3[:, :, 0:G]])
        e4 = product("e4", [d3[:, :, 1 : G + 1], d2[:, :, 2 : G + 2], d1[:, :, 3 : G + 3]])
        k2 = const.tile([P, U, NK], F32)
        nc.vector.tensor_copy(out=k2[:, :, 0:G], in_=c0[:])
        nc.vector.tensor_copy(out=k2[:, :, G:NK], in_=e4[:, :, NEG:G])
        ksq = const.tile([P, U, NK], F32)
        nc.vector.reciprocal(out=ksq[:], in_=k2[:])
        kap = const.tile([P, U, NK], F32)
        nc.scalar.activation(out=kap[:], in_=ksq[:], func=ACT.Sqrt)
        tps_next = [turn_x(xs0, u) for u in range(U)]
        rk = const.tile([P, U, NK], F32)
        nc.vector.reciprocal(out=rk[:], in_=kap[:])
        nc.vector.tensor_mul(out=ksq[:], in0=rk[:], in1=ksq[:])
        nc.vector.tensor_add(out=ksq[:], in0=ksq[:], in1=kap[:])
        nc.vector.tensor_scalar_mul(out=ksq[:], in0=ksq[:], scalar1=0.5)
        nb = const.tile([P, U, NK], F32)
        nc.vector.tensor_mul(out=nb[:], in0=ksq[:], in1=neg_g[:])
        nc.vector.tensor_mul(out=k2[:], in0=ksq[:], in1=ksq[:])
        nc.vector.reciprocal(out=k2[:], in_=k2[:])
        c1 = product("c1", [d1[:, :, 0:G], d1[:, :, 1 : G + 1], d2[:, :, 1 : G + 1], d3[:, :, 1 : G + 1]])
        nc.vector.reciprocal(out=c1[:], in_=c1[:])
        nc.vector.tensor_mul(out=c1[:], in0=c1[:], in1=d4[:])
        nc.vector.tensor_mul(out=c1[:], in0=c1[:], in1=k2[:, :, 1 : G + 1])
        nc.vector.reciprocal(out=e4[:], in_=e4[:])
        nc.vector.tensor_scalar_mul(out=e4[:], in0=e4[:], scalar1=-1.0)
        nc.vector.tensor_mul(out=e4[:], in0=e4[:], in1=k2[:, :, 4 : G + 4])
        e3 = product("e3", [d3[:, :, 0:G], d2[:, :, 1 : G + 1], d1[:, :, 2 : G + 2], d1[:, :, 3 : G + 3]])
        nc.vector.reciprocal(out=e3[:], in_=e3[:])
        nc.vector.tensor_mul(out=e3[:], in0=e3[:], in1=d4[:])
        nc.vector.tensor_scalar_mul(out=e3[:], in0=e3[:], scalar1=-1.0)
        nc.vector.tensor_mul(out=e3[:], in0=e3[:], in1=k2[:, :, 3 : G + 3])

        zero = const.tile([P, 1], F32)
        gate_out = const.tile([P, 1], F32)
        w_codes = const.tile([P, NPL * O], U32, align_bytes=64)
        w_scales = const.tile([P, NPL * O], U8, align_bytes=64)

        def multiply_weights():
            msp = wprep.tile([P, U, O], F32)
            nc.gpsimd.tensor_mul(out=msp[:], in0=mask_sb[:], in1=sp_sb[:])
            coef_v = coef_sb[:].rearrange("p u (o k) -> p k o u", k=G)
            products = []
            for first, count in ((0, 8), (8, 4)):
                w_grouped = grp_pool.tile([P, NB, U], BF16, tag="grp", align_bytes=64)
                w_flat = w_grouped[:].rearrange("p b u -> p (b u)")
                for n in range(count):
                    plane = first + n
                    dst = w_flat[:, n * O * U : (n + 1) * O * U].rearrange("p (o u) -> p o u", u=U)
                    if plane < G:
                        nc.gpsimd.tensor_tensor(
                            out=dst, in0=coef_v[:, plane, :, :], in1=msp[:].rearrange("p u o -> p o u"), op=ALU.mult
                        )
                    else:
                        nc.gpsimd.tensor_tensor(
                            out=dst,
                            in0=mask_sb[:].rearrange("p u o -> p o u"),
                            in1=base_sb[:].rearrange("p u o -> p o u"),
                            op=ALU.mult,
                        )
                products.append((first, count, w_flat))
            return products

        def quantise_weights(products):
            for first, count, w_flat in products:
                nc.vector.quantize_mx(
                    out=w_codes[:, first * O : (first + count) * O].bitcast(FP8X4),
                    scales=w_scales[:, first * O : (first + count) * O],
                    in_=w_flat[:, 0 : count * O * U],
                )

        def by_runs_dst(grouped, lo, hi):
            return grouped[:, lo:hi, :].rearrange("p (c r) u -> p c u r", r=RUN)

        def by_runs_src(plane, lo, hi):
            return plane[:, :, lo:hi].rearrange("p u (c r) -> p c u r", r=RUN)

        def quantise_and_multiply(grouped, plane, acc):
            codes = q_pool.tile([P, NB], U32, align_bytes=64)
            scales = q_pool.tile([P, NB], U8, align_bytes=64)
            nc.vector.quantize_mx(
                out=codes[:].bitcast(FP8X4), scales=scales[:], in_=grouped[:].rearrange("p b u -> p (b u)")
            )
            w_cols = slice(plane * O, (plane + 1) * O)
            for h in range(NB // HALF):
                cols = slice(h * HALF, (h + 1) * HALF)
                nc.tensor.matmul_mx(
                    out=acc[h][:],
                    lhsT=w_codes[:, w_cols].bitcast(FP8X4),
                    lhsT_scale=w_scales[:, w_cols],
                    rhs=codes[:, cols].bitcast(FP8X4),
                    rhs_scale=scales[:, cols],
                    start=(plane == 0),
                    stop=(plane == G - 1),
                )

        def regroup(plane_tile, sc):
            grouped = grp_pool.tile([P, NB, U], BF16, tag="grp", align_bytes=64)
            if sc < NB:
                nc.vector.tensor_scalar_max(
                    out=by_runs_dst(grouped, sc, NB), in0=by_runs_src(plane_tile, sc, NB), scalar1=0.0
                )
            return grouped

        def regroup_on_scalar(plane_tile, grouped, sc):
            nc.scalar.activation(
                out=by_runs_dst(grouped, 0, sc), in_=by_runs_src(plane_tile, 0, sc), func=ACT.Relu
            )

        def empty_sums(acc):
            out_t = o_pool.tile([P, NB], F32)
            nc.scalar.copy(out=out_t[:, 0:HALF], in_=acc[0][:])
            nc.vector.tensor_copy(out=out_t[:, HALF:NB], in_=acc[1][:])
            turned = []
            for h in range(NB // HALF):
                ot = ot_psum.tile([P, 4, O], F32)
                for q in range(4):
                    n = h * 4 + q
                    nc.tensor.transpose(ot[:, q, :], out_t[:, n * P : (n + 1) * P], ident_f[:])
                turned.append(ot)
            return turned

        def store(turned, c):
            out_sb = o_pool.tile([P, NT, O], F32)
            nc.scalar.copy(out=out_sb[:, 0:4, :], in_=turned[0][:])
            nc.vector.tensor_copy(out=out_sb[:, 4:8, :], in_=turned[1][:])
            nc.sync.dma_start(out=out[c * NB : (c + 1) * NB, :].rearrange("(p n) o -> p n o", n=NT), in_=out_sb[:])

        def squares(t, j, source=None):
            sqs = []
            for u in range(U):
                if source is not None:
                    nc.scalar.copy(out=t[:, u, :], in_=source[u][:])
                sq = sq_pool.tile([P, NB], F32)
                nc.scalar.activation(
                    out=sq[:], in_=t[:, u, :], func=ACT.Square, bias=nb[:, u, j : j + 1], scale=ksq[:, u, j : j + 1]
                )
                sqs.append(sq)
            return sqs

        def flat(tile, lo, hi):
            return tile[:].rearrange("p u b -> p (u b)")[:, lo:hi]

        def combine(engine, lo, hi, job):
            half, in0, in1, op, woven = job
            if woven:
                lo, hi = lo // U, hi // U
                engine.tensor_tensor(
                    out=by_runs_dst(half, lo, hi), in0=by_runs_src(in0, lo, hi), in1=by_runs_src(in1, lo, hi), op=op
                )
            else:
                engine.tensor_tensor(out=flat(half, lo, hi), in0=flat(in0, lo, hi), in1=flat(in1, lo, hi), op=op)

        ALL = U * NB
        to_left = None
        on_gpsimd = {}
        merges = {}
        to_regroup = None
        to_quantise = []
        to_empty = None
        to_store = None
        t = t_pool.tile([P, U, NB], BF16)
        tps = tps_next
        sqs = squares(t, 0, tps)
        s_prev = None
        right_in = None
        lefts = {}
        accs = {}

        for step in range(NCH * NK + 5):
            c, j = divmod(step, NK)
            live = c < NCH
            left_job = to_left
            to_left = None
            if live and j == 5:
                acc0 = acc_psum.tile([P, HALF], F32)
                acc1 = acc_psum.tile([P, HALF], F32)
                accs[c] = [acc0, acc1]
            if live and j == 0 and c + 1 < NCH:
                xs_next = load_x(c + 1)

            if left_job is not None:
                combine(nc.gpsimd, 0, GX, left_job)
            if step in on_gpsimd:
                nc.gpsimd.tensor_scalar(
                    out=gate_out[:], in0=zero[:], scalar1=1.0, scalar2=0.0, op0=ALU.mult, op1=ALU.add
                )
                lo, hi, job = on_gpsimd[step]
                combine(nc.gpsimd, lo, hi, job)

            if live:
                s_cur = s_pool.tile([P, U, NB], F32, tag="s")
                for u in range(U):
                    nc.vector.scalar_tensor_tensor(
                        out=s_cur[:, u, :], in0=tps[u][:], scalar=g[:, u, j : j + 1], in1=sqs[u][:],
                        op0=ALU.subtract, op1=ALU.mult,
                    )
                if j == NK - 1 and c + 1 < NCH:
                    tps_next = [turn_x(xs_next, u) for u in range(U)]
                if left_job is not None:
                    combine(nc.vector, GX, ALL, left_job)
                if j >= 4:
                    k = j - 4
                    wait = 0
                    if k < NEG:
                        right = right_pool.tile([P, U, NB], BF16, tag="right", align_bytes=64)
                        for u in range(U):
                            nc.vector.scalar_tensor_tensor(
                                out=right[:, u, :], in0=s_cur[:, u, :], scalar=e4[:, u, k : k + 1], in1=right_in[:, u, :],
                                op0=ALU.mult, op1=ALU.subtract,
                            )
                    else:
                        right = right_pool.tile([P, NB, U], BF16, tag="right", align_bytes=64)
                        job = (right, s_cur, right_in, ALU.add, True)
                        lo = 0
                        if k >= LATE:
                            wait = 1
                            if step + 1 < NCH * NK:
                                lo = GX
                                on_gpsimd[step + 1] = (0, GX, job)
                                if k == G - 1:
                                    lo = ALL
                                    wait = 2
                                    on_gpsimd[step + 2] = (GX, ALL, job)
                        if lo < ALL:
                            combine(nc.vector, lo, ALL, job)
                    merges[step + wait] = (right, k, c)
            if step == 0:
                products = multiply_weights()
            if step == 3:
                quantise_weights(products)
            quantised = to_quantise
            to_quantise = []
            for grouped, plane, c_of in quantised:
                quantise_and_multiply(grouped, plane, accs[c_of])
            made = None
            if step in merges:
                right_of, plane, c_of = merges[step]
                nc.vector.tensor_tensor(
                    out=right_of[:], in0=lefts[c_of, plane][:], in1=right_of[:], op=ALU.max if plane < NEG else ALU.min
                )
                made = (right_of, plane, c_of)
            if step + 1 in on_gpsimd:
                nc.vector.memset(zero[:], 0.0)
            rest = None
            if to_regroup is not None:
                plane_tile, plane, c_of = to_regroup
                share = BUSY
                if plane < NEG:
                    grouped = regroup(plane_tile, share)
                    to_quantise.append((grouped, plane, c_of))
                    rest = (plane_tile, grouped, share)
                else:
                    flipped = grp_pool.tile([P, NB, U], BF16, tag="grp", align_bytes=64)
                    if live or plane == G - 1:
                        nc.vector.tensor_scalar(
                            out=flipped[:], in0=plane_tile[:], scalar1=-1.0, scalar2=0.0, op0=ALU.mult, op1=ALU.max
                        )
                    else:
                        nc.scalar.activation(out=flipped[:], in_=plane_tile[:], func=ACT.Relu, scale=-1.0)
                    to_quantise.append((flipped, plane, c_of))
            to_regroup = made

            if live:
                if j == G + 2:
                    base_grouped = base_pool.tile([P, NB, U], BF16, align_bytes=64)
                    nc.scalar.activation(out=by_runs_dst(base_grouped, 0, NB), in_=by_runs_src(t, 0, NB), func=ACT.Silu)
                    to_quantise.append((base_grouped, G, c))
                if j == NK - 1 and c + 1 < NCH:
                    t = t_pool.tile([P, U, NB], BF16)
                    tps = tps_next
                    sqs = squares(t, 0, tps)
                elif j < NK - 1:
                    sqs = squares(t, j + 1)
                if 1 <= j <= G:
                    k = j - 1
                    left_in = in_pool.tile([P, U, NB], F32)
                    for u in range(U):
                        nc.scalar.activation(
                            out=left_in[:, u, :], in_=s_cur[:, u, :], func=ACT.Relu, scale=c1[:, u, k : k + 1]
                        )
                    if k < NEG:
                        left = left_pool.tile([P, U, NB], BF16, tag="left")
                        to_left = (left, s_prev, left_in, ALU.subtract, False)
                    else:
                        left = left_pool.tile([P, NB, U], BF16, tag="left")
                        to_left = (left, left_in, s_prev, ALU.subtract, True)
                    lefts[c, k] = left
                if 3 <= j <= G + 2:
                    k = j - 3
                    right_in = in_pool.tile([P, U, NB], F32, bufs=2)
                    for u in range(U):
                        nc.scalar.activation(
                            out=right_in[:, u, :], in_=s_cur[:, u, :], func=ACT.Relu, scale=e3[:, u, k : k + 1]
                        )
                if rest is not None:
                    regroup_on_scalar(*rest)
                s_prev = s_cur
            if to_store is not None:
                store(to_store[0], to_store[1])
                to_store = None
            if to_empty is not None:
                to_store = (empty_sums(accs[to_empty]), to_empty)
                to_empty = None
            for grouped, plane, c_of in quantised:
                if plane == G - 1:
                    to_empty = c_of
